import numpy as np
import ml_dtypes


def mxq(x, axis, fmt="e4m3"):
    dtype, down = {"e4m3": (ml_dtypes.float8_e4m3fn, 7), "e5m2": (ml_dtypes.float8_e5m2, 14)}[fmt]
    v = np.moveaxis(np.asarray(x, np.float32).astype(ml_dtypes.bfloat16).astype(np.float64), axis, -1)
    blocks = v.reshape(v.shape[:-1] + (-1, 32))
    amax = np.abs(blocks).max(-1, keepdims=True)
    byte = np.maximum(np.where(amax > 0, np.frexp(amax)[1] - 1 + 127, 0) - down, 1)
    scale = np.exp2(byte - 127.0)
    codes = (blocks / scale).astype(np.float32).astype(dtype).astype(np.float64)
    return np.moveaxis((codes * scale).reshape(v.shape), -1, axis)


WIDE = False


def mx_kscale(k):
    if not WIDE:
        return np.ones(k)
    levels = np.array([10, -10, 5, -5, 0])
    a = np.random.permutation(np.resize(levels, k // 512 * 4)).reshape(k // 512, 4)
    idx = np.arange(k)
    return np.exp2(a[idx // 512, idx % 128 // 32])


BF16 = ml_dtypes.bfloat16


def bf(x):
    return np.asarray(x, np.float32).astype(BF16)


def f64(x):
    return np.asarray(x).astype(np.float64)


B, S, D_MODEL, D_POS, H, D_FF = 512, 8, 512, 512, 4, 2048
DPP = D_POS // H
DPH = D_MODEL // H


def setup_inputs():
    s = mx_kscale(D_MODEL)
    gq = np.exp2(np.random.uniform(-1.0, 1.0, (S, H, B, 1)))
    gk = np.exp2(np.random.uniform(-1.0, 1.0, (S, H, B, 1)))
    return {"q_pos": bf(np.random.standard_normal((S, H, B, DPP)) * gq * 3.0 / np.sqrt(DPP)),
            "k_pos": bf(np.random.standard_normal((S, H, B, DPP)) * gk * 3.0 / np.sqrt(DPP)),
            "x_grp": bf(np.random.standard_normal((S, B, D_MODEL)) * s),
            "Wv": bf(np.random.standard_normal((D_MODEL, D_MODEL)) * 0.5 / np.sqrt(D_MODEL) / s),
            "bv": bf(np.random.standard_normal(D_MODEL) * 10.0 / B)}


def reference(q_pos, k_pos, x_grp, Wv, bv):
    v = (mxq(f64(x_grp), 2, "e4m3") @ mxq(f64(Wv).T, 0, "e4m3")) + f64(bv)
    v = v.reshape(S, B, H, DPH).transpose(0, 2, 1, 3)
    q2 = np.sum(f64(q_pos) * f64(q_pos), axis=-1)
    k2 = np.sum(f64(k_pos) * f64(k_pos), axis=-1)
    d2 = q2[..., :, None] + k2[..., None, :] - 2.0 * (f64(q_pos) @ f64(k_pos).transpose(0, 1, 3, 2))
    dist = np.sqrt(np.maximum(d2, 1e-12)) + 1.0
    scores = 1.0 / dist
    causal = np.triu(np.ones((B, B), bool), k=1)
    scores = np.where(causal, 0.0, scores)
    o = mxq(scores, 3, "e4m3") @ mxq(v, 2, "e4m3")
    return o.transpose(0, 2, 1, 3).reshape(S, B, D_MODEL)

@@ -1,0 +1,260 @@
+from contextlib import ExitStack
+
+import concourse.mybir as mybir
+from concourse.masks import make_identity
+
+F32 = mybir.dt.float32
+BF16 = mybir.dt.bfloat16
+U32 = mybir.dt.uint32
+U8 = mybir.dt.uint8
+FP8X4 = mybir.dt.float8_e4m3fn_x4
+ACT = mybir.ActivationFunctionType
+ALU = mybir.AluOpType
+
+P = 128
+GROUPS = 8
+HEADS = 4
+TOKENS = 512
+TILES = TOKENS // P
+MODEL = 512
+PACK = 4
+EPS = 1e-12
+MASKED = 1.0e30
+BATCH = 8
+ALL_HEADS = GROUPS * HEADS
+
+FLOPS = 3 * 2 * GROUPS * TOKENS * MODEL * MODEL
+
+
+def tile_networklayer_pb_t_kernel(tc, q_pos, k_pos, x_grp, Wv, bv, out):
+    nc = tc.nc
+    with ExitStack() as ctx:
+        const = ctx.enter_context(tc.tile_pool(name="const", bufs=1))
+        raw = ctx.enter_context(tc.tile_pool(name="raw", bufs=3))
+        stage = ctx.enter_context(tc.tile_pool(name="stage", bufs=2))
+        norms = ctx.enter_context(tc.tile_pool(name="norms", bufs=BATCH + 4))
+        turned = ctx.enter_context(tc.tile_pool(name="turned", bufs=BATCH + 2))
+        dist = ctx.enter_context(tc.tile_pool(name="dist", bufs=BATCH + 1))
+        wcode = ctx.enter_context(tc.tile_pool(name="wcode", bufs=BATCH + 1))
+        vcode = ctx.enter_context(tc.tile_pool(name="vcode", bufs=6))
+        result = ctx.enter_context(tc.tile_pool(name="result", bufs=2))
+        psum_qk = ctx.enter_context(tc.psum_pool(name="psum_qk", bufs=4))
+        psum_tp = ctx.enter_context(tc.psum_pool(name="psum_tp", bufs=2))
+        psum_mx = ctx.enter_context(tc.psum_pool(name="psum_mx", bufs=2))
+
+        ident_b = const.tile([P, P], BF16, name="ident_b")
+        make_identity(nc, ident_b[:])
+        ident_f = const.tile([P, P], F32, name="ident_f")
+        make_identity(nc, ident_f[:])
+        bias = const.tile([P, MODEL], BF16, name="bias")
+        nc.sync.dma_start(out=bias[:], in_=bv.partition_broadcast(P))
+        squares = const.tile([P, P], BF16, name="squares")
+        weights = [
+            const.tile([P, TOKENS, PACK], BF16, name="weights%d" % i, align_bytes=64)
+            for i in range(3)
+        ]
+        for w_tile in weights:
+            nc.vector.memset(w_tile[:], 0.0)
+        wv_codes = const.tile([P, MODEL], U32, name="wv_codes", align_bytes=64)
+        wv_scales = const.tile([P, MODEL], U8, name="wv_scales", align_bytes=64)
+
+        q_raw = {}
+        k_raw = {}
+        x_raw = {}
+        x_codes = {}
+        x_scales = {}
+        v_grouped = {}
+        v_codes = {}
+        v_scales = {}
+        half_norms = {}
+        qk_turned = {}
+        half_d2 = {}
+        w_codes = {}
+        w_scales = {}
+        o_rows = {}
+
+        def load_group(g):
+            q_raw[g] = raw.tile([P, HEADS * TILES, P], BF16, name="q_raw")
+            nc.sync.dma_start(out=q_raw[g][:], in_=q_pos[g].rearrange("h (u p) d -> p (h u) d", p=P))
+            k_raw[g] = raw.tile([P, HEADS * TILES, P], BF16, name="k_raw")
+            nc.sync.dma_start(out=k_raw[g][:], in_=k_pos[g].rearrange("h (u p) d -> p (h u) d", p=P))
+            x_raw[g] = raw.tile([P, TILES, MODEL], BF16, name="x_raw")
+            nc.sync.dma_start(out=x_raw[g][:], in_=x_grp[g].rearrange("(t p) k -> p t k", p=P))
+
+        def quantise_rows(rows, codes, scales):
+            words = rows[:].bitcast(F32)
+            grouped = stage.tile([P, TOKENS * PACK], BF16, name="grouped", align_bytes=64)
+            grouped_words = grouped[:].bitcast(F32).rearrange("p (r u) -> p r u", u=2)
+            for pair in range(TILES // 2):
+                tp = psum_tp.tile([P, 2, 2 * P], F32, name="tp_words", tag="tp")
+                for i in range(2):
+                    for u in range(2):
+                        nc.tensor.transpose(
+                            out=tp[:, u, i * P : (i + 1) * P],
+                            in_=words[:, 2 * pair + i, u * P : (u + 1) * P],
+                            identity=ident_f[:],
+                        )
+                nc.vector.tensor_copy(
+                    out=grouped_words[:, 2 * pair * P : 2 * (pair + 1) * P, :],
+                    in_=tp[:].rearrange("p u r -> p r u"),
+                )
+            nc.vector.quantize_mx(out=codes[:].bitcast(FP8X4), scales=scales[:], in_=grouped[:])
+
+        def prepare(n):
+            g, h = divmod(n, HEADS)
+            if h == 0:
+                x_codes[g] = stage.tile([P, TOKENS], U32, name="x_codes", align_bytes=64)
+                x_scales[g] = stage.tile([P, TOKENS], U8, name="x_scales", align_bytes=64)
+                quantise_rows(x_raw[g], x_codes[g], x_scales[g])
+                v_grouped[g] = stage.tile([P, MODEL, PACK], BF16, name="v_grouped", align_bytes=64)
+            sums = norms.tile([P, 2 * TILES], F32, name="sums")
+            tp = psum_tp.tile([P, 2 * TILES, P], BF16, name="tp_qk", tag="tp")
+            for i, source in enumerate((q_raw[g], k_raw[g])):
+                for u in range(TILES):
+                    rows = source[:, h * TILES + u, :]
+                    col = i * TILES + u
+                    nc.scalar.activation(out=squares[:], in_=rows, func=ACT.Square, accum_out=sums[:, col : col + 1])
+                    nc.tensor.transpose(out=tp[:, col, :], in_=rows, identity=ident_b[:])
+            half_norms[n] = norms.tile([P, 2 * TILES], F32, name="half_norms")
+            nc.vector.tensor_scalar_mul(out=half_norms[n][:], in0=sums[:], scalar1=-0.5)
+            qk_turned[n] = turned.tile([P, 2, TOKENS], BF16, name="qk_turned")
+            nc.vector.tensor_copy(
+                out=qk_turned[n][:].rearrange("p a b -> p (a b)"), in_=tp[:].rearrange("p i b -> p (i b)")
+            )
+            cols = slice(h * P, (h + 1) * P)
+            acc = psum_mx.tile([P, TILES, P], F32, name="v_acc", tag="mx")
+            for t in range(TILES):
+                rows = slice(t * P, (t + 1) * P)
+                nc.tensor.matmul_mx(
+                    out=acc[:, t, :],
+                    lhsT=x_codes[g][:, rows].bitcast(FP8X4),
+                    lhsT_scale=x_scales[g][:, rows],
+                    rhs=wv_codes[:, cols].bitcast(FP8X4),
+                    rhs_scale=wv_scales[:, cols],
+                    start=True,
+                    stop=True,
+                )
+            nc.vector.tensor_tensor(
+                out=v_grouped[g][:, cols, :],
+                in0=acc[:].rearrange("p t j -> p j t"),
+                in1=bias[:, cols].unsqueeze(2).to_broadcast([P, P, PACK]),
+                op=ALU.add,
+            )
+            if h == HEADS - 1:
+                v_codes[g] = vcode.tile([P, MODEL], U32, name="v_codes", align_bytes=64)
+                v_scales[g] = vcode.tile([P, MODEL], U8, name="v_scales", align_bytes=64)
+                nc.vector.quantize_mx(
+                    out=v_codes[g][:].bitcast(FP8X4),
+                    scales=v_scales[g][:],
+                    in_=v_grouped[g][:].rearrange("p j t -> p (j t)"),
+                )
+                if g + 3 < GROUPS:
+                    load_group(g + 3)
+
+        def scores(n):
+            q_t = qk_turned[n][:, 0, :]
+            k_t = qk_turned[n][:, 1, :]
+            half_d2[n] = dist.tile([P, TILES, TOKENS], F32, name="half_d2")
+            for t in range(TILES):
+                width = TOKENS - t * P
+                acc = psum_qk.tile([P, TOKENS], F32, name="qk_acc", tag="qk")
+                nc.tensor.matmul(
+                    out=acc[:, 0:width], lhsT=k_t[:, t * P : (t + 1) * P], rhs=q_t[:, t * P : TOKENS], start=True, stop=False
+                )
+                for u in range(t, TILES):
+                    nc.tensor.matmul(
+                        out=acc[:, (u - t) * P : (u - t + 1) * P],
+                        lhsT=half_norms[n][:, u : u + 1].to_broadcast([P, P]),
+                        rhs=ident_f[:],
+                        is_transpose=True,
+                        start=False,
+                        stop=(u == TILES - 1),
+                    )
+                nc.vector.tensor_scalar(
+                    out=half_d2[n][:, t, 0:width],
+                    in0=acc[:, 0:width],
+                    scalar1=half_norms[n][:, TILES + t : TILES + t + 1],
+                    scalar2=-0.5 * EPS,
+                    op0=ALU.add,
+                    op1=ALU.min,
+                )
+
+        def logarithm(n):
+            for t in range(TILES):
+                row = half_d2[n][:, t, 0 : TOKENS - t * P]
+                nc.scalar.activation(out=row, in_=row, func=ACT.Ln, scale=-2.0)
+                diagonal = half_d2[n][:, t, 0:P]
+                nc.gpsimd.affine_select(
+                    out=diagonal,
+                    in_=diagonal,
+                    pattern=[[1, P]],
+                    compare_op=ALU.is_ge,
+                    fill=MASKED,
+                    base=0,
+                    channel_multiplier=-1,
+                )
+
+        def sigmoid(n):
+            w_tile = weights[n % 3]
+            flat = half_d2[n][:].rearrange("p t b -> p (t b)")
+            step = TOKENS - P
+            for u in range(TILES):
+                column = flat[:, u * P : u * P + (u + 1) * step].rearrange("p (t x) -> p t x", x=step)[:, :, 0:P]
+                nc.scalar.activation(
+                    out=w_tile[:, u * P : (u + 1) * P, 0 : u + 1],
+                    in_=column.rearrange("p t b -> p b t"),
+                    func=ACT.Sigmoid,
+                    scale=-0.5,
+                )
+            w_codes[n] = wcode.tile([P, TOKENS], U32, name="w_codes", align_bytes=64)
+            w_scales[n] = wcode.tile([P, TOKENS], U8, name="w_scales", align_bytes=64)
+            nc.vector.quantize_mx(
+                out=w_codes[n][:].bitcast(FP8X4), scales=w_scales[n][:], in_=w_tile[:].rearrange("p b t -> p (b t)")
+            )
+
+        def finish(n):
+            g, h = divmod(n, HEADS)
+            cols = slice(h * P, (h + 1) * P)
+            if h == 0:
+                o_rows[g] = result.tile([P, TILES, MODEL], F32, name="o_rows")
+            acc = psum_mx.tile([P, TILES, P], F32, name="o_acc", tag="mx")
+            for u in range(TILES):
+                rows = slice(u * P, (u + 1) * P)
+                nc.tensor.matmul_mx(
+                    out=acc[:, u, :],
+                    lhsT=w_codes[n][:, rows].bitcast(FP8X4),
+                    lhsT_scale=w_scales[n][:, rows],
+                    rhs=v_codes[g][:, cols].bitcast(FP8X4),
+                    rhs_scale=v_scales[g][:, cols],
+                    start=True,
+                    stop=True,
+                )
+            nc.vector.tensor_copy(out=o_rows[g][:, :, cols], in_=acc[:])
+            if h == HEADS - 1:
+                nc.sync.dma_start(out=out[g].rearrange("(u p) j -> p u j", p=P), in_=o_rows[g][:])
+
+        wv_raw = raw.tile([P, TILES, MODEL], BF16, name="x_raw")
+        nc.sync.dma_start(out=wv_raw[:], in_=Wv.rearrange("(t p) k -> p t k", p=P))
+        for g in range(3):
+            load_group(g)
+
+        with tc.manual_schedule():
+            quantise_rows(wv_raw, wv_codes, wv_scales)
+            for n in range(BATCH):
+                prepare(n)
+                scores(n)
+            for first in range(0, ALL_HEADS, BATCH):
+                last_batch = first + BATCH == ALL_HEADS
+                for n in range(first, first + BATCH):
+                    logarithm(n)
+                    if first > 0:
+                        finish(n - BATCH)
+                    if not last_batch:
+                        prepare(n + BATCH)
+                for n in range(first, first + BATCH):
+                    sigmoid(n)
+                    if not last_batch:
+                        scores(n + BATCH)
+                    elif n > first:
+                        finish(n - 1)
+            finish(ALL_HEADS - 1)

@@ -47,7 +47,6 @@ def tile_networklayer_pb_t_kernel(tc, q_pos, k_pos, x_grp, Wv, bv, out):
         ident_f = const.tile([P, P], F32, name="ident_f")
         make_identity(nc, ident_f[:])
         bias = const.tile([P, MODEL], BF16, name="bias")
-        nc.sync.dma_start(out=bias[:], in_=bv.partition_broadcast(P))
         squares = const.tile([P, P], BF16, name="squares")
         weights = [
             const.tile([P, TOKENS, PACK], BF16, name="weights%d" % i, align_bytes=64)
@@ -114,7 +113,7 @@ def tile_networklayer_pb_t_kernel(tc, q_pos, k_pos, x_grp, Wv, bv, out):
                     rows = source[:, h * TILES + u, :]
                     col = i * TILES + u
                     nc.scalar.activation(out=squares[:], in_=rows, func=ACT.Square, accum_out=sums[:, col : col + 1])
-                    nc.tensor.transpose(out=tp[:, col, :], in_=rows, identity=ident_b[:])
+                    nc.tensor.matmul(out=tp[:, col, :], lhsT=rows, rhs=ident_b[:], start=True, stop=True)
             half_norms[n] = norms.tile([P, 2 * TILES], F32, name="half_norms")
             nc.vector.tensor_scalar_mul(out=half_norms[n][:], in0=sums[:], scalar1=-0.5)
             qk_turned[n] = turned.tile([P, 2, TOKENS], BF16, name="qk_turned")
@@ -235,8 +234,10 @@ def tile_networklayer_pb_t_kernel(tc, q_pos, k_pos, x_grp, Wv, bv, out):
 
         wv_raw = raw.tile([P, TILES, MODEL], BF16, name="x_raw")
         nc.sync.dma_start(out=wv_raw[:], in_=Wv.rearrange("(t p) k -> p t k", p=P))
-        for g in range(3):
-            load_group(g)
+        load_group(0)
+        nc.sync.dma_start(out=bias[:], in_=bv.partition_broadcast(P))
+        load_group(1)
+        load_group(2)
 
         with tc.manual_schedule():
             quantise_rows(wv_raw, wv_codes, wv_scales)

@@ -18,10 +18,10 @@ TOKENS = 512
 TILES = TOKENS // P
 MODEL = 512
 PACK = 4
-EPS = 1e-12
-MASKED = 1.0e30
-BATCH = 8
+INV_EPS = 1.0e6
+MASKED = -(2.0**95)
 ALL_HEADS = GROUPS * HEADS
+W_BUFS = 3
 
 FLOPS = 3 * 2 * GROUPS * TOKENS * MODEL * MODEL
 
@@ -32,11 +32,11 @@ def tile_networklayer_pb_t_kernel(tc, q_pos, k_pos, x_grp, Wv, bv, out):
         const = ctx.enter_context(tc.tile_pool(name="const", bufs=1))
         raw = ctx.enter_context(tc.tile_pool(name="raw", bufs=3))
         stage = ctx.enter_context(tc.tile_pool(name="stage", bufs=2))
-        norms = ctx.enter_context(tc.tile_pool(name="norms", bufs=BATCH + 4))
-        turned = ctx.enter_context(tc.tile_pool(name="turned", bufs=BATCH + 2))
-        dist = ctx.enter_context(tc.tile_pool(name="dist", bufs=BATCH + 1))
-        wcode = ctx.enter_context(tc.tile_pool(name="wcode", bufs=BATCH + 1))
-        vcode = ctx.enter_context(tc.tile_pool(name="vcode", bufs=6))
+        norms = ctx.enter_context(tc.tile_pool(name="norms", bufs=6))
+        turned = ctx.enter_context(tc.tile_pool(name="turned", bufs=3))
+        dist = ctx.enter_context(tc.tile_pool(name="dist", bufs=3))
+        wcode = ctx.enter_context(tc.tile_pool(name="wcode", bufs=2))
+        vcode = ctx.enter_context(tc.tile_pool(name="vcode", bufs=3))
         result = ctx.enter_context(tc.tile_pool(name="result", bufs=2))
         psum_qk = ctx.enter_context(tc.psum_pool(name="psum_qk", bufs=4))
         psum_tp = ctx.enter_context(tc.psum_pool(name="psum_tp", bufs=2))
@@ -46,11 +46,22 @@ def tile_networklayer_pb_t_kernel(tc, q_pos, k_pos, x_grp, Wv, bv, out):
         make_identity(nc, ident_b[:])
         ident_f = const.tile([P, P], F32, name="ident_f")
         make_identity(nc, ident_f[:])
+        mask = const.tile([P, P], F32, name="mask")
+        nc.gpsimd.memset(mask[:], 0.0)
+        nc.gpsimd.affine_select(
+            out=mask[:],
+            in_=mask[:],
+            pattern=[[-1, P]],
+            compare_op=ALU.is_ge,
+            fill=MASKED,
+            base=0,
+            channel_multiplier=1,
+        )
         bias = const.tile([P, MODEL], BF16, name="bias")
         squares = const.tile([P, P], BF16, name="squares")
         weights = [
             const.tile([P, TOKENS, PACK], BF16, name="weights%d" % i, align_bytes=64)
-            for i in range(3)
+            for i in range(W_BUFS)
         ]
         for w_tile in weights:
             nc.vector.memset(w_tile[:], 0.0)
@@ -60,72 +71,106 @@ def tile_networklayer_pb_t_kernel(tc, q_pos, k_pos, x_grp, Wv, bv, out):
         q_raw = {}
         k_raw = {}
         x_raw = {}
+        x_grouped = {}
         x_codes = {}
         x_scales = {}
         v_grouped = {}
         v_codes = {}
         v_scales = {}
+        norm_sums = {}
         half_norms = {}
+        qk_psum = {}
         qk_turned = {}
-        half_d2 = {}
+        scores_psum = {}
+        work = {}
         w_codes = {}
         w_scales = {}
+        v_psum = {}
+        o_psum = {}
         o_rows = {}
 
-        def load_group(g):
+        def load_x(g):
+            x_raw[g] = raw.tile([P, TILES, MODEL], BF16, name="x_raw")
+            nc.sync.dma_start(out=x_raw[g][:], in_=x_grp[g].rearrange("(t p) k -> p t k", p=P))
+
+        def load_qk(g):
             q_raw[g] = raw.tile([P, HEADS * TILES, P], BF16, name="q_raw")
             nc.sync.dma_start(out=q_raw[g][:], in_=q_pos[g].rearrange("h (u p) d -> p (h u) d", p=P))
             k_raw[g] = raw.tile([P, HEADS * TILES, P], BF16, name="k_raw")
             nc.sync.dma_start(out=k_raw[g][:], in_=k_pos[g].rearrange("h (u p) d -> p (h u) d", p=P))
-            x_raw[g] = raw.tile([P, TILES, MODEL], BF16, name="x_raw")
-            nc.sync.dma_start(out=x_raw[g][:], in_=x_grp[g].rearrange("(t p) k -> p t k", p=P))
 
-        def quantise_rows(rows, codes, scales):
+        def turn_rows(rows, grouped, pair):
             words = rows[:].bitcast(F32)
-            grouped = stage.tile([P, TOKENS * PACK], BF16, name="grouped", align_bytes=64)
             grouped_words = grouped[:].bitcast(F32).rearrange("p (r u) -> p r u", u=2)
-            for pair in range(TILES // 2):
-                tp = psum_tp.tile([P, 2, 2 * P], F32, name="tp_words", tag="tp")
-                for i in range(2):
-                    for u in range(2):
-                        nc.tensor.transpose(
-                            out=tp[:, u, i * P : (i + 1) * P],
-                            in_=words[:, 2 * pair + i, u * P : (u + 1) * P],
-                            identity=ident_f[:],
-                        )
-                nc.vector.tensor_copy(
-                    out=grouped_words[:, 2 * pair * P : 2 * (pair + 1) * P, :],
-                    in_=tp[:].rearrange("p u r -> p r u"),
-                )
-            nc.vector.quantize_mx(out=codes[:].bitcast(FP8X4), scales=scales[:], in_=grouped[:])
+            tp = psum_tp.tile([P, 2, 2 * P], F32, name="tp_words", tag="tp")
+            for i in range(2):
+                for u in range(2):
+                    nc.tensor.transpose(
+                        out=tp[:, u, i * P : (i + 1) * P],
+                        in_=words[:, 2 * pair + i, u * P : (u + 1) * P],
+                        identity=ident_f[:],
+                    )
+            nc.vector.tensor_copy(
+                out=grouped_words[:, 2 * pair * P : 2 * (pair + 1) * P, :],
+                in_=tp[:].rearrange("p u r -> p r u"),
+            )
 
-        def prepare(n):
+        def quantise(codes, scales, grouped):
+            nc.vector.quantize_mx(out=codes.bitcast(FP8X4), scales=scales, in_=grouped)
+
+        def turn_x(g, pair):
+            if pair == 0:
+                x_grouped[g] = stage.tile([P, TOKENS * PACK], BF16, name="x_grouped", align_bytes=64)
+            turn_rows(x_raw[g], x_grouped[g], pair)
+
+        def quantise_x(g):
+            x_codes[g] = stage.tile([P, TOKENS], U32, name="x_codes", align_bytes=64)
+            x_scales[g] = stage.tile([P, TOKENS], U8, name="x_scales", align_bytes=64)
+            quantise(x_codes[g][:], x_scales[g][:], x_grouped[g][:])
+
+        def square(n):
             g, h = divmod(n, HEADS)
-            if h == 0:
-                x_codes[g] = stage.tile([P, TOKENS], U32, name="x_codes", align_bytes=64)
-                x_scales[g] = stage.tile([P, TOKENS], U8, name="x_scales", align_bytes=64)
-                quantise_rows(x_raw[g], x_codes[g], x_scales[g])
-                v_grouped[g] = stage.tile([P, MODEL, PACK], BF16, name="v_grouped", align_bytes=64)
-            sums = norms.tile([P, 2 * TILES], F32, name="sums")
-            tp = psum_tp.tile([P, 2 * TILES, P], BF16, name="tp_qk", tag="tp")
+            norm_sums[n] = norms.tile([P, 2 * TILES], F32, name="norm_sums")
             for i, source in enumerate((q_raw[g], k_raw[g])):
                 for u in range(TILES):
-                    rows = source[:, h * TILES + u, :]
                     col = i * TILES + u
-                    nc.scalar.activation(out=squares[:], in_=rows, func=ACT.Square, accum_out=sums[:, col : col + 1])
-                    nc.tensor.matmul(out=tp[:, col, :], lhsT=rows, rhs=ident_b[:], start=True, stop=True)
+                    nc.scalar.activation(
+                        out=squares[:],
+                        in_=source[:, h * TILES + u, :],
+                        func=ACT.Square,
+                        accum_out=norm_sums[n][:, col : col + 1],
+                    )
+
+        def halve(n):
             half_norms[n] = norms.tile([P, 2 * TILES], F32, name="half_norms")
-            nc.vector.tensor_scalar_mul(out=half_norms[n][:], in0=sums[:], scalar1=-0.5)
+            nc.vector.tensor_scalar_mul(out=half_norms[n][:], in0=norm_sums[n][:], scalar1=-0.5)
+
+        def turn_qk(n):
+            g, h = divmod(n, HEADS)
+            qk_psum[n] = psum_tp.tile([P, 2 * TILES, P], BF16, name="tp_qk", tag="tp")
+            for i, source in enumerate((q_raw[g], k_raw[g])):
+                for u in range(TILES):
+                    nc.tensor.transpose(
+                        out=qk_psum[n][:, i * TILES + u, :],
+                        in_=source[:, h * TILES + u, :],
+                        identity=ident_b[:],
+                    )
+
+        def copy_qk(n):
             qk_turned[n] = turned.tile([P, 2, TOKENS], BF16, name="qk_turned")
             nc.vector.tensor_copy(
-                out=qk_turned[n][:].rearrange("p a b -> p (a b)"), in_=tp[:].rearrange("p i b -> p (i b)")
+                out=qk_turned[n][:].rearrange("p a b -> p (a b)"),
+                in_=qk_psum[n][:].rearrange("p i b -> p (i b)"),
             )
+
+        def project(n):
+            g, h = divmod(n, HEADS)
             cols = slice(h * P, (h + 1) * P)
-            acc = psum_mx.tile([P, TILES, P], F32, name="v_acc", tag="mx")
+            v_psum[n] = psum_mx.tile([P, TILES, P], F32, name="v_acc", tag="mx")
             for t in range(TILES):
                 rows = slice(t * P, (t + 1) * P)
                 nc.tensor.matmul_mx(
-                    out=acc[:, t, :],
+                    out=v_psum[n][:, t, :],
                     lhsT=x_codes[g][:, rows].bitcast(FP8X4),
                     lhsT_scale=x_scales[g][:, rows],
                     rhs=wv_codes[:, cols].bitcast(FP8X4),
@@ -133,32 +178,42 @@ def tile_networklayer_pb_t_kernel(tc, q_pos, k_pos, x_grp, Wv, bv, out):
                     start=True,
                     stop=True,
                 )
+
+        def add_bias(n):
+            g, h = divmod(n, HEADS)
+            cols = slice(h * P, (h + 1) * P)
+            v_grouped[n] = stage.tile([P, P, PACK], BF16, name="v_grouped", align_bytes=64)
             nc.vector.tensor_tensor(
-                out=v_grouped[g][:, cols, :],
-                in0=acc[:].rearrange("p t j -> p j t"),
+                out=v_grouped[n][:],
+                in0=v_psum[n][:].rearrange("p t j -> p j t"),
                 in1=bias[:, cols].unsqueeze(2).to_broadcast([P, P, PACK]),
                 op=ALU.add,
             )
-            if h == HEADS - 1:
+
+        def quantise_v(n):
+            g, h = divmod(n, HEADS)
+            cols = slice(h * P, (h + 1) * P)
+            if h == 0:
                 v_codes[g] = vcode.tile([P, MODEL], U32, name="v_codes", align_bytes=64)
                 v_scales[g] = vcode.tile([P, MODEL], U8, name="v_scales", align_bytes=64)
-                nc.vector.quantize_mx(
-                    out=v_codes[g][:].bitcast(FP8X4),
-                    scales=v_scales[g][:],
-                    in_=v_grouped[g][:].rearrange("p j t -> p (j t)"),
-                )
-                if g + 3 < GROUPS:
-                    load_group(g + 3)
+            quantise(v_codes[g][:, cols], v_scales[g][:, cols], v_grouped[n][:].rearrange("p j t -> p (j t)"))
+
+        def block(n, t):
+            width = TOKENS - t * P
+            first = 0 if t != 3 else TOKENS - P
+            return scores_psum[n][(0, 1, 2, 1)[t]][:, first : first + width]
 
         def scores(n):
             q_t = qk_turned[n][:, 0, :]
             k_t = qk_turned[n][:, 1, :]
-            half_d2[n] = dist.tile([P, TILES, TOKENS], F32, name="half_d2")
+            scores_psum[n] = [psum_qk.tile([P, TOKENS], F32, name="qk_acc", tag="qk") for bank in range(3)]
             for t in range(TILES):
-                width = TOKENS - t * P
-                acc = psum_qk.tile([P, TOKENS], F32, name="qk_acc", tag="qk")
+                acc = block(n, t)
                 nc.tensor.matmul(
-                    out=acc[:, 0:width], lhsT=k_t[:, t * P : (t + 1) * P], rhs=q_t[:, t * P : TOKENS], start=True, stop=False
+                    out=acc, lhsT=k_t[:, t * P : (t + 1) * P], rhs=q_t[:, t * P : TOKENS], start=True, stop=False
+                )
+                nc.tensor.matmul(
+                    out=acc[:, 0:P], lhsT=mask[:], rhs=ident_f[:], is_transpose=True, start=False, stop=False
                 )
                 for u in range(t, TILES):
                     nc.tensor.matmul(
@@ -169,58 +224,63 @@ def tile_networklayer_pb_t_kernel(tc, q_pos, k_pos, x_grp, Wv, bv, out):
                         start=False,
                         stop=(u == TILES - 1),
                     )
-                nc.vector.tensor_scalar(
-                    out=half_d2[n][:, t, 0:width],
-                    in0=acc[:, 0:width],
-                    scalar1=half_norms[n][:, TILES + t : TILES + t + 1],
-                    scalar2=-0.5 * EPS,
-                    op0=ALU.add,
-                    op1=ALU.min,
-                )
 
-        def logarithm(n):
+        def inverse_root(n):
+            work[n] = dist.tile([P, TILES, TOKENS], F32, name="work")
             for t in range(TILES):
-                row = half_d2[n][:, t, 0 : TOKENS - t * P]
-                nc.scalar.activation(out=row, in_=row, func=ACT.Ln, scale=-2.0)
-                diagonal = half_d2[n][:, t, 0:P]
-                nc.gpsimd.affine_select(
-                    out=diagonal,
-                    in_=diagonal,
-                    pattern=[[1, P]],
-                    compare_op=ALU.is_ge,
-                    fill=MASKED,
-                    base=0,
-                    channel_multiplier=-1,
+                row = work[n][:, t, t * P : TOKENS]
+                nc.scalar.activation(
+                    out=row,
+                    in_=block(n, t),
+                    func=ACT.Abs_reciprocal_sqrt,
+                    scale=-2.0,
+                    bias=norm_sums[n][:, TILES + t : TILES + t + 1],
+                )
+                nc.gpsimd.tensor_scalar(out=row, in0=row, scalar1=INV_EPS, scalar2=0.5, op0=ALU.min, op1=ALU.add)
+                nc.vector.scalar_tensor_tensor(
+                    out=row,
+                    in0=block(n, t),
+                    scalar=half_norms[n][:, TILES + t : TILES + t + 1],
+                    in1=row,
+                    op0=ALU.add,
+                    op1=ALU.mult,
                 )
 
-        def sigmoid(n):
-            w_tile = weights[n % 3]
-            flat = half_d2[n][:].rearrange("p t b -> p (t b)")
-            step = TOKENS - P
+        def weigh(n):
+            w_tile = weights[n % W_BUFS]
             for u in range(TILES):
-                column = flat[:, u * P : u * P + (u + 1) * step].rearrange("p (t x) -> p t x", x=step)[:, :, 0:P]
+                cols = slice(u * P, (u + 1) * P)
                 nc.scalar.activation(
-                    out=w_tile[:, u * P : (u + 1) * P, 0 : u + 1],
-                    in_=column.rearrange("p t b -> p b t"),
-                    func=ACT.Sigmoid,
-                    scale=-0.5,
+                    out=w_tile[:, cols, 0 : u + 1],
+                    in_=work[n][:, 0 : u + 1, cols].rearrange("p t b -> p b t"),
+                    func=ACT.Abs_reciprocal_sqrt,
+                    scale=-4.0,
+                    bias=1.0,
                 )
-            w_codes[n] = wcode.tile([P, TOKENS], U32, name="w_codes", align_bytes=64)
-            w_scales[n] = wcode.tile([P, TOKENS], U8, name="w_scales", align_bytes=64)
-            nc.vector.quantize_mx(
-                out=w_codes[n][:].bitcast(FP8X4), scales=w_scales[n][:], in_=w_tile[:].rearrange("p b t -> p (b t)")
+            first = w_tile[:, 0:P, 0]
+            nc.gpsimd.affine_select(
+                out=first,
+                in_=first,
+                pattern=[[1, P]],
+                compare_op=ALU.is_ge,
+                fill=0.0,
+                base=0,
+                channel_multiplier=-1,
             )
 
-        def finish(n):
+        def quantise_w(n):
+            w_codes[n] = wcode.tile([P, TOKENS], U32, name="w_codes", align_bytes=64)
+            w_scales[n] = wcode.tile([P, TOKENS], U8, name="w_scales", align_bytes=64)
+            quantise(w_codes[n][:], w_scales[n][:], weights[n % W_BUFS][:].rearrange("p b t -> p (b t)"))
+
+        def attend(n):
             g, h = divmod(n, HEADS)
             cols = slice(h * P, (h + 1) * P)
-            if h == 0:
-                o_rows[g] = result.tile([P, TILES, MODEL], F32, name="o_rows")
-            acc = psum_mx.tile([P, TILES, P], F32, name="o_acc", tag="mx")
+            o_psum[n] = psum_mx.tile([P, TILES, P], F32, name="o_acc", tag="mx")
             for u in range(TILES):
                 rows = slice(u * P, (u + 1) * P)
                 nc.tensor.matmul_mx(
-                    out=acc[:, u, :],
+                    out=o_psum[n][:, u, :],
                     lhsT=w_codes[n][:, rows].bitcast(FP8X4),
                     lhsT_scale=w_scales[n][:, rows],
                     rhs=v_codes[g][:, cols].bitcast(FP8X4),
@@ -228,34 +288,66 @@ def tile_networklayer_pb_t_kernel(tc, q_pos, k_pos, x_grp, Wv, bv, out):
                     start=True,
                     stop=True,
                 )
-            nc.vector.tensor_copy(out=o_rows[g][:, :, cols], in_=acc[:])
+
+        def copy_out(n):
+            g, h = divmod(n, HEADS)
+            cols = slice(h * P, (h + 1) * P)
+            if h == 0:
+                o_rows[g] = result.tile([P, TILES, MODEL], F32, name="o_rows")
+            nc.vector.tensor_copy(out=o_rows[g][:, :, cols], in_=o_psum[n][:])
             if h == HEADS - 1:
                 nc.sync.dma_start(out=out[g].rearrange("(u p) j -> p u j", p=P), in_=o_rows[g][:])
 
         wv_raw = raw.tile([P, TILES, MODEL], BF16, name="x_raw")
         nc.sync.dma_start(out=wv_raw[:], in_=Wv.rearrange("(t p) k -> p t k", p=P))
-        load_group(0)
+        load_qk(0)
+        load_x(0)
         nc.sync.dma_start(out=bias[:], in_=bv.partition_broadcast(P))
-        load_group(1)
-        load_group(2)
+        load_x(1)
+        load_qk(1)
+        load_qk(2)
+
+        def valid(n):
+            return 0 <= n < ALL_HEADS
 
         with tc.manual_schedule():
-            quantise_rows(wv_raw, wv_codes, wv_scales)
-            for n in range(BATCH):
-                prepare(n)
-                scores(n)
-            for first in range(0, ALL_HEADS, BATCH):
-                last_batch = first + BATCH == ALL_HEADS
-                for n in range(first, first + BATCH):
-                    logarithm(n)
-                    if first > 0:
-                        finish(n - BATCH)
-                    if not last_batch:
-                        prepare(n + BATCH)
-                for n in range(first, first + BATCH):
-                    sigmoid(n)
-                    if not last_batch:
-                        scores(n + BATCH)
-                    elif n > first:
-                        finish(n - 1)
-            finish(ALL_HEADS - 1)
+            wv_grouped = stage.tile([P, TOKENS * PACK], BF16, name="x_grouped", align_bytes=64)
+            for pair in range(2):
+                turn_rows(wv_raw, wv_grouped, pair)
+            quantise(wv_codes[:], wv_scales[:], wv_grouped[:])
+            for pair in range(2):
+                turn_x(0, pair)
+            quantise_x(0)
+            load_x(2)
+            for i in range(-4, ALL_HEADS + 2):
+                if valid(i - 1):
+                    quantise_w(i - 1)
+                if valid(i + 3):
+                    halve(i + 3)
+                    turn_qk(i + 3)
+                    copy_qk(i + 3)
+                if valid(i - 1):
+                    attend(i - 1)
+                    copy_out(i - 1)
+                if valid(i + 3):
+                    project(i + 3)
+                if valid(i + 1):
+                    inverse_root(i + 1)
+                if valid(i):
+                    weigh(i)
+                if valid(i + 2):
+                    quantise_v(i + 2)
+                    scores(i + 2)
+                if valid(i + 3):
+                    add_bias(i + 3)
+                    g, h = divmod(i + 3, HEADS)
+                    if g + 1 < GROUPS:
+                        if h in (1, 2):
+                            turn_x(g + 1, h - 1)
+                        if h == 3:
+                            quantise_x(g + 1)
+                            if g + 3 < GROUPS:
+                                load_x(g + 3)
+                                load_qk(g + 3)
+                if valid(i + 4):
+                    square(i + 4)

@@ -18,7 +18,11 @@ TOKENS = 512
 TILES = TOKENS // P
 MODEL = 512
 PACK = 4
+EPS = 1.0e-12
 INV_EPS = 1.0e6
+SPLIT = 3
+SLOT = 32
+BY_MATMUL = [0, 1, 3]
 MASKED = -(2.0**95)
 ALL_HEADS = GROUPS * HEADS
 W_BUFS = 3
@@ -30,9 +34,9 @@ def tile_networklayer_pb_t_kernel(tc, q_pos, k_pos, x_grp, Wv, bv, out):
     nc = tc.nc
     with ExitStack() as ctx:
         const = ctx.enter_context(tc.tile_pool(name="const", bufs=1))
-        raw = ctx.enter_context(tc.tile_pool(name="raw", bufs=3))
+        raw = ctx.enter_context(tc.tile_pool(name="raw", bufs=4))
         stage = ctx.enter_context(tc.tile_pool(name="stage", bufs=2))
-        norms = ctx.enter_context(tc.tile_pool(name="norms", bufs=6))
+        norms = ctx.enter_context(tc.tile_pool(name="norms", bufs=4))
         turned = ctx.enter_context(tc.tile_pool(name="turned", bufs=3))
         dist = ctx.enter_context(tc.tile_pool(name="dist", bufs=3))
         wcode = ctx.enter_context(tc.tile_pool(name="wcode", bufs=2))
@@ -65,12 +69,23 @@ def tile_networklayer_pb_t_kernel(tc, q_pos, k_pos, x_grp, Wv, bv, out):
         ]
         for w_tile in weights:
             nc.vector.memset(w_tile[:], 0.0)
+        split_q = [const.tile([P, TILES, P], BF16, name="split_q%d" % i) for i in range(2)]
+        split_k = [const.tile([P, HEADS, TILES, P], BF16, name="split_k%d" % i) for i in range(2)]
+        for i in range(2):
+            nc.gpsimd.memset(split_q[i][:], 0.0)
+            nc.gpsimd.memset(split_k[i][:], 0.0)
+            for h in range(HEADS):
+                nc.gpsimd.memset(split_q[i][:, :, h * SLOT + SPLIT : h * SLOT + 2 * SPLIT], -0.5)
+                nc.gpsimd.memset(split_k[i][:, h, :, h * SLOT : h * SLOT + SPLIT], -0.5)
         wv_codes = const.tile([P, MODEL], U32, name="wv_codes", align_bytes=64)
         wv_scales = const.tile([P, MODEL], U8, name="wv_scales", align_bytes=64)
 
         q_raw = {}
         k_raw = {}
         x_raw = {}
+        q_side = {}
+        k_side = {}
+        norm_psum = {}
         x_grouped = {}
         x_codes = {}
         x_scales = {}
@@ -130,20 +145,58 @@ def tile_networklayer_pb_t_kernel(tc, q_pos, k_pos, x_grp, Wv, bv, out):
 
         def square(n):
             g, h = divmod(n, HEADS)
-            norm_sums[n] = norms.tile([P, 2 * TILES], F32, name="norm_sums")
+            if h == 0:
+                norm_sums[g] = norms.tile([P, HEADS, 2, TILES], F32, name="norm_sums")
             for i, source in enumerate((q_raw[g], k_raw[g])):
                 for u in range(TILES):
-                    col = i * TILES + u
                     nc.scalar.activation(
                         out=squares[:],
                         in_=source[:, h * TILES + u, :],
                         func=ACT.Square,
-                        accum_out=norm_sums[n][:, col : col + 1],
+                        accum_out=norm_sums[g][:, h, i, u : u + 1],
                     )
 
-        def halve(n):
-            half_norms[n] = norms.tile([P, 2 * TILES], F32, name="half_norms")
-            nc.vector.tensor_scalar_mul(out=half_norms[n][:], in0=norm_sums[n][:], scalar1=-0.5)
+        def split_norms(g):
+            sums = norm_sums[g]
+            half_norms[g] = norms.tile([P, HEADS, 2, TILES], F32, name="half_norms")
+            nc.gpsimd.tensor_scalar(
+                out=half_norms[g][:], in0=sums[:], scalar1=-0.5, scalar2=0.0, op0=ALU.mult, op1=ALU.add
+            )
+            terms = norms.tile([P, SPLIT, HEADS, 2, TILES], BF16, name="terms")
+            rest = norms.tile([P, HEADS, 2, TILES], F32, name="rest")
+            nc.gpsimd.tensor_copy(out=terms[:, 0], in_=sums[:])
+            nc.gpsimd.tensor_tensor(out=rest[:], in0=sums[:], in1=terms[:, 0], op=ALU.subtract)
+            nc.gpsimd.tensor_copy(out=terms[:, 1], in_=rest[:])
+            nc.gpsimd.tensor_tensor(out=terms[:, 2], in0=rest[:], in1=terms[:, 1], op=ALU.subtract)
+            for h in range(HEADS):
+                nc.gpsimd.tensor_copy(
+                    out=split_q[g % 2][:, :, h * SLOT : h * SLOT + SPLIT],
+                    in_=terms[:, :, h, 0, :].rearrange("p i u -> p u i"),
+                )
+                nc.gpsimd.tensor_copy(
+                    out=split_k[g % 2][:, h, :, h * SLOT + SPLIT : h * SLOT + 2 * SPLIT],
+                    in_=terms[:, :, h, 1, :].rearrange("p i u -> p u i"),
+                )
+
+        def turn_norms(n):
+            g, h = divmod(n, HEADS)
+            norm_psum[n] = psum_tp.tile([P, 2, TILES, P], BF16, name="tp_norms", tag="tp")
+            for slot, t in enumerate(BY_MATMUL):
+                nc.tensor.transpose(out=norm_psum[n][:, 0, slot, :], in_=split_k[g % 2][:, h, t, :], identity=ident_b[:])
+            if h == 0:
+                for u in range(TILES):
+                    nc.tensor.transpose(out=norm_psum[n][:, 1, u, :], in_=split_q[g % 2][:, u, :], identity=ident_b[:])
+
+        def copy_norms(n):
+            g, h = divmod(n, HEADS)
+            slots = len(BY_MATMUL)
+            k_side[n] = turned.tile([P, slots, P], BF16, name="k_side")
+            nc.vector.tensor_copy(out=k_side[n][:], in_=norm_psum[n][:, 0, 0:slots, :])
+            if h == 0:
+                q_side[g] = turned.tile([P, TOKENS], BF16, name="q_side")
+                nc.vector.tensor_copy(
+                    out=q_side[g][:], in_=norm_psum[n][:, 1].rearrange("p u b -> p (u b)")
+                )
 
         def turn_qk(n):
             g, h = divmod(n, HEADS)
@@ -204,6 +257,7 @@ def tile_networklayer_pb_t_kernel(tc, q_pos, k_pos, x_grp, Wv, bv, out):
             return scores_psum[n][(0, 1, 2, 1)[t]][:, first : first + width]
 
         def scores(n):
+            g, h = divmod(n, HEADS)
             q_t = qk_turned[n][:, 0, :]
             k_t = qk_turned[n][:, 1, :]
             scores_psum[n] = [psum_qk.tile([P, TOKENS], F32, name="qk_acc", tag="qk") for bank in range(3)]
@@ -215,36 +269,49 @@ def tile_networklayer_pb_t_kernel(tc, q_pos, k_pos, x_grp, Wv, bv, out):
                 nc.tensor.matmul(
                     out=acc[:, 0:P], lhsT=mask[:], rhs=ident_f[:], is_transpose=True, start=False, stop=False
                 )
-                for u in range(t, TILES):
+                if t in BY_MATMUL:
                     nc.tensor.matmul(
-                        out=acc[:, (u - t) * P : (u - t + 1) * P],
-                        lhsT=half_norms[n][:, u : u + 1].to_broadcast([P, P]),
-                        rhs=ident_f[:],
-                        is_transpose=True,
-                        start=False,
-                        stop=(u == TILES - 1),
+                        out=acc, lhsT=k_side[n][:, BY_MATMUL.index(t), :], rhs=q_side[g][:, t * P : TOKENS], start=False, stop=True
                     )
+                else:
+                    for u in range(t, TILES):
+                        nc.tensor.matmul(
+                            out=acc[:, (u - t) * P : (u - t + 1) * P],
+                            lhsT=half_norms[g][:, h, 0, u : u + 1].to_broadcast([P, P]),
+                            rhs=ident_f[:],
+                            is_transpose=True,
+                            start=False,
+                            stop=(u == TILES - 1),
+                        )
 
         def inverse_root(n):
+            g, h = divmod(n, HEADS)
             work[n] = dist.tile([P, TILES, TOKENS], F32, name="work")
-            for t in range(TILES):
-                row = work[n][:, t, t * P : TOKENS]
+            for t in (2, 0, 1, 3):
                 nc.scalar.activation(
-                    out=row,
+                    out=work[n][:, t, t * P : TOKENS],
                     in_=block(n, t),
                     func=ACT.Abs_reciprocal_sqrt,
                     scale=-2.0,
-                    bias=norm_sums[n][:, TILES + t : TILES + t + 1],
+                    bias=EPS if t in BY_MATMUL else norm_sums[g][:, h, 1, t : t + 1],
                 )
-                nc.gpsimd.tensor_scalar(out=row, in0=row, scalar1=INV_EPS, scalar2=0.5, op0=ALU.min, op1=ALU.add)
-                nc.vector.scalar_tensor_tensor(
-                    out=row,
-                    in0=block(n, t),
-                    scalar=half_norms[n][:, TILES + t : TILES + t + 1],
-                    in1=row,
-                    op0=ALU.add,
-                    op1=ALU.mult,
-                )
+            row = work[n][:, 2, 2 * P : TOKENS]
+            nc.vector.tensor_scalar(out=row, in0=row, scalar1=INV_EPS, scalar2=0.5, op0=ALU.min, op1=ALU.add)
+            for t in (0, 2, 1, 3):
+                row = work[n][:, t, t * P : TOKENS]
+                if t in BY_MATMUL:
+                    nc.vector.scalar_tensor_tensor(
+                        out=row, in0=row, scalar=0.5, in1=block(n, t), op0=ALU.add, op1=ALU.mult
+                    )
+                else:
+                    nc.vector.scalar_tensor_tensor(
+                        out=row,
+                        in0=block(n, t),
+                        scalar=half_norms[g][:, h, 1, t : t + 1],
+                        in1=row,
+                        op0=ALU.add,
+                        op1=ALU.mult,
+                    )
 
         def weigh(n):
             w_tile = weights[n % W_BUFS]
@@ -299,33 +366,37 @@ def tile_networklayer_pb_t_kernel(tc, q_pos, k_pos, x_grp, Wv, bv, out):
                 nc.sync.dma_start(out=out[g].rearrange("(u p) j -> p u j", p=P), in_=o_rows[g][:])
 
         wv_raw = raw.tile([P, TILES, MODEL], BF16, name="x_raw")
-        nc.sync.dma_start(out=wv_raw[:], in_=Wv.rearrange("(t p) k -> p t k", p=P))
         load_qk(0)
+        nc.sync.dma_start(out=wv_raw[:], in_=Wv.rearrange("(t p) k -> p t k", p=P))
         load_x(0)
         nc.sync.dma_start(out=bias[:], in_=bv.partition_broadcast(P))
-        load_x(1)
         load_qk(1)
+        load_x(1)
         load_qk(2)
+        load_x(2)
+        load_qk(3)
 
         def valid(n):
             return 0 <= n < ALL_HEADS
 
         with tc.manual_schedule():
-            wv_grouped = stage.tile([P, TOKENS * PACK], BF16, name="x_grouped", align_bytes=64)
-            for pair in range(2):
-                turn_rows(wv_raw, wv_grouped, pair)
-            quantise(wv_codes[:], wv_scales[:], wv_grouped[:])
-            for pair in range(2):
-                turn_x(0, pair)
-            quantise_x(0)
-            load_x(2)
-            for i in range(-4, ALL_HEADS + 2):
+            for i in range(-9, ALL_HEADS + 2):
+                if i == -5:
+                    wv_grouped = stage.tile([P, TOKENS * PACK], BF16, name="x_grouped", align_bytes=64)
+                    for pair in range(2):
+                        turn_rows(wv_raw, wv_grouped, pair)
+                    for pair in range(2):
+                        turn_x(0, pair)
+                    quantise(wv_codes[:], wv_scales[:], wv_grouped[:])
+                    quantise_x(0)
+                    load_x(3)
                 if valid(i - 1):
                     quantise_w(i - 1)
                 if valid(i + 3):
-                    halve(i + 3)
                     turn_qk(i + 3)
+                    turn_norms(i + 3)
                     copy_qk(i + 3)
+                    copy_norms(i + 3)
                 if valid(i - 1):
                     attend(i - 1)
                     copy_out(i - 1)
@@ -335,6 +406,8 @@ def tile_networklayer_pb_t_kernel(tc, q_pos, k_pos, x_grp, Wv, bv, out):
                     inverse_root(i + 1)
                 if valid(i):
                     weigh(i)
+                if (i + 5) % HEADS == 0 and valid(i + 5):
+                    split_norms((i + 5) // HEADS)
                 if valid(i + 2):
                     quantise_v(i + 2)
                     scores(i + 2)
@@ -346,8 +419,8 @@ def tile_networklayer_pb_t_kernel(tc, q_pos, k_pos, x_grp, Wv, bv, out):
                             turn_x(g + 1, h - 1)
                         if h == 3:
                             quantise_x(g + 1)
-                            if g + 3 < GROUPS:
-                                load_x(g + 3)
-                                load_qk(g + 3)
-                if valid(i + 4):
-                    square(i + 4)
+                            if g + 4 < GROUPS:
+                                load_qk(g + 4)
+                                load_x(g + 4)
+                if valid(i + 9):
+                    square(i + 9)

@@ -62,7 +62,7 @@ def tile_networklayer_pb_t_kernel(tc, q_pos, k_pos, x_grp, Wv, bv, out):
             channel_multiplier=1,
         )
         bias = const.tile([P, MODEL], BF16, name="bias")
-        squares = const.tile([P, P], BF16, name="squares")
+        squares = const.tile([P, 2, HEADS * TILES // 2, P], BF16, name="squares")
         weights = [
             const.tile([P, TOKENS, PACK], BF16, name="weights%d" % i, align_bytes=64)
             for i in range(W_BUFS)
@@ -150,7 +150,7 @@ def tile_networklayer_pb_t_kernel(tc, q_pos, k_pos, x_grp, Wv, bv, out):
             for i, source in enumerate((q_raw[g], k_raw[g])):
                 for u in range(TILES):
                     nc.scalar.activation(
-                        out=squares[:],
+                        out=squares[:, n % 2, i * TILES + u, :],
                         in_=source[:, h * TILES + u, :],
                         func=ACT.Square,
                         accum_out=norm_sums[g][:, h, i, u : u + 1],

@@ -26,6 +26,7 @@ BY_MATMUL = [0, 1, 3]
 MASKED = -(2.0**95)
 ALL_HEADS = GROUPS * HEADS
 W_BUFS = 3
+RUN = 4
 
 FLOPS = 3 * 2 * GROUPS * TOKENS * MODEL * MODEL
 
@@ -318,8 +319,8 @@ def tile_networklayer_pb_t_kernel(tc, q_pos, k_pos, x_grp, Wv, bv, out):
             for u in range(TILES):
                 cols = slice(u * P, (u + 1) * P)
                 nc.scalar.activation(
-                    out=w_tile[:, cols, 0 : u + 1],
-                    in_=work[n][:, 0 : u + 1, cols].rearrange("p t b -> p b t"),
+                    out=w_tile[:, cols, 0 : u + 1].rearrange("p (c i) t -> p c t i", i=RUN),
+                    in_=work[n][:, 0 : u + 1, cols].rearrange("p t (c i) -> p c t i", i=RUN),
                     func=ACT.Abs_reciprocal_sqrt,
                     scale=-4.0,
                     bias=1.0,

@@ -26,6 +26,7 @@ BY_MATMUL = [0, 1, 3]
 MASKED = -(2.0**95)
 ALL_HEADS = GROUPS * HEADS
 W_BUFS = 3
+SQUARES_AHEAD = 9
 RUN = 4
 
 FLOPS = 3 * 2 * GROUPS * TOKENS * MODEL * MODEL
@@ -40,12 +41,12 @@ def tile_networklayer_pb_t_kernel(tc, q_pos, k_pos, x_grp, Wv, bv, out):
         norms = ctx.enter_context(tc.tile_pool(name="norms", bufs=4))
         turned = ctx.enter_context(tc.tile_pool(name="turned", bufs=3))
         dist = ctx.enter_context(tc.tile_pool(name="dist", bufs=3))
-        wcode = ctx.enter_context(tc.tile_pool(name="wcode", bufs=2))
+        wcode = ctx.enter_context(tc.tile_pool(name="wcode", bufs=3))
         vcode = ctx.enter_context(tc.tile_pool(name="vcode", bufs=3))
         result = ctx.enter_context(tc.tile_pool(name="result", bufs=2))
         psum_qk = ctx.enter_context(tc.psum_pool(name="psum_qk", bufs=4))
-        psum_tp = ctx.enter_context(tc.psum_pool(name="psum_tp", bufs=2))
-        psum_mx = ctx.enter_context(tc.psum_pool(name="psum_mx", bufs=2))
+        psum_tp = ctx.enter_context(tc.psum_pool(name="psum_tp", bufs=1))
+        psum_mx = ctx.enter_context(tc.psum_pool(name="psum_mx", bufs=1))
 
         ident_b = const.tile([P, P], BF16, name="ident_b")
         make_identity(nc, ident_b[:])
@@ -63,7 +64,7 @@ def tile_networklayer_pb_t_kernel(tc, q_pos, k_pos, x_grp, Wv, bv, out):
             channel_multiplier=1,
         )
         bias = const.tile([P, MODEL], BF16, name="bias")
-        squares = const.tile([P, 2, HEADS * TILES // 2, P], BF16, name="squares")
+        squares = const.tile([P, 2, 2 * TILES, P], F32, name="squares")
         weights = [
             const.tile([P, TOKENS, PACK], BF16, name="weights%d" % i, align_bytes=64)
             for i in range(W_BUFS)
@@ -87,6 +88,7 @@ def tile_networklayer_pb_t_kernel(tc, q_pos, k_pos, x_grp, Wv, bv, out):
         q_side = {}
         k_side = {}
         norm_psum = {}
+        x_psum = {}
         x_grouped = {}
         x_codes = {}
         x_scales = {}
@@ -115,10 +117,9 @@ def tile_networklayer_pb_t_kernel(tc, q_pos, k_pos, x_grp, Wv, bv, out):
             k_raw[g] = raw.tile([P, HEADS * TILES, P], BF16, name="k_raw")
             nc.sync.dma_start(out=k_raw[g][:], in_=k_pos[g].rearrange("h (u p) d -> p (h u) d", p=P))
 
-        def turn_rows(rows, grouped, pair):
+        def turn_rows(rows, pair, pool, tag):
             words = rows[:].bitcast(F32)
-            grouped_words = grouped[:].bitcast(F32).rearrange("p (r u) -> p r u", u=2)
-            tp = psum_tp.tile([P, 2, 2 * P], F32, name="tp_words", tag="tp")
+            tp = pool.tile([P, 2, 2 * P], F32, name="tp_words", tag=tag)
             for i in range(2):
                 for u in range(2):
                     nc.tensor.transpose(
@@ -126,6 +127,10 @@ def tile_networklayer_pb_t_kernel(tc, q_pos, k_pos, x_grp, Wv, bv, out):
                         in_=words[:, 2 * pair + i, u * P : (u + 1) * P],
                         identity=ident_f[:],
                     )
+            return tp
+
+        def group_rows(tp, grouped, pair):
+            grouped_words = grouped[:].bitcast(F32).rearrange("p (r u) -> p r u", u=2)
             nc.vector.tensor_copy(
                 out=grouped_words[:, 2 * pair * P : 2 * (pair + 1) * P, :],
                 in_=tp[:].rearrange("p u r -> p r u"),
@@ -135,9 +140,12 @@ def tile_networklayer_pb_t_kernel(tc, q_pos, k_pos, x_grp, Wv, bv, out):
             nc.vector.quantize_mx(out=codes.bitcast(FP8X4), scales=scales, in_=grouped)
 
         def turn_x(g, pair):
+            x_psum[g] = turn_rows(x_raw[g], pair, psum_tp, "tp_side")
+
+        def group_x(g, pair):
             if pair == 0:
                 x_grouped[g] = stage.tile([P, TOKENS * PACK], BF16, name="x_grouped", align_bytes=64)
-            turn_rows(x_raw[g], x_grouped[g], pair)
+            group_rows(x_psum[g], x_grouped[g], pair)
 
         def quantise_x(g):
             x_codes[g] = stage.tile([P, TOKENS], U32, name="x_codes", align_bytes=64)
@@ -150,12 +158,15 @@ def tile_networklayer_pb_t_kernel(tc, q_pos, k_pos, x_grp, Wv, bv, out):
                 norm_sums[g] = norms.tile([P, HEADS, 2, TILES], F32, name="norm_sums")
             for i, source in enumerate((q_raw[g], k_raw[g])):
                 for u in range(TILES):
-                    nc.scalar.activation(
-                        out=squares[:, n % 2, i * TILES + u, :],
-                        in_=source[:, h * TILES + u, :],
-                        func=ACT.Square,
-                        accum_out=norm_sums[g][:, h, i, u : u + 1],
-                    )
+                    rows = source[:, h * TILES + u, :]
+                    unused = squares[:, n % 2, i * TILES + u, :]
+                    total = norm_sums[g][:, h, i, u : u + 1]
+                    if g == 0 and i == 0:
+                        nc.vector.scalar_tensor_tensor(
+                            out=unused, in0=rows, scalar=1.0, in1=rows, op0=ALU.mult, op1=ALU.mult, accum_out=total
+                        )
+                    else:
+                        nc.scalar.activation(out=unused, in_=rows, func=ACT.Square, accum_out=total)
 
         def split_norms(g):
             sums = norm_sums[g]
@@ -181,7 +192,7 @@ def tile_networklayer_pb_t_kernel(tc, q_pos, k_pos, x_grp, Wv, bv, out):
 
         def turn_norms(n):
             g, h = divmod(n, HEADS)
-            norm_psum[n] = psum_tp.tile([P, 2, TILES, P], BF16, name="tp_norms", tag="tp")
+            norm_psum[n] = psum_tp.tile([P, 2, TILES, P], BF16, name="tp_norms", tag="tp_side")
             for slot, t in enumerate(BY_MATMUL):
                 nc.tensor.transpose(out=norm_psum[n][:, 0, slot, :], in_=split_k[g % 2][:, h, t, :], identity=ident_b[:])
             if h == 0:
@@ -201,7 +212,7 @@ def tile_networklayer_pb_t_kernel(tc, q_pos, k_pos, x_grp, Wv, bv, out):
 
         def turn_qk(n):
             g, h = divmod(n, HEADS)
-            qk_psum[n] = psum_tp.tile([P, 2 * TILES, P], BF16, name="tp_qk", tag="tp")
+            qk_psum[n] = psum_tp.tile([P, 2 * TILES, P], BF16, name="tp_qk", tag="tp_qk")
             for i, source in enumerate((q_raw[g], k_raw[g])):
                 for u in range(TILES):
                     nc.tensor.transpose(
@@ -220,7 +231,7 @@ def tile_networklayer_pb_t_kernel(tc, q_pos, k_pos, x_grp, Wv, bv, out):
         def project(n):
             g, h = divmod(n, HEADS)
             cols = slice(h * P, (h + 1) * P)
-            v_psum[n] = psum_mx.tile([P, TILES, P], F32, name="v_acc", tag="mx")
+            v_psum[n] = psum_mx.tile([P, TILES, P], F32, name="v_acc")
             for t in range(TILES):
                 rows = slice(t * P, (t + 1) * P)
                 nc.tensor.matmul_mx(
@@ -257,12 +268,13 @@ def tile_networklayer_pb_t_kernel(tc, q_pos, k_pos, x_grp, Wv, bv, out):
             first = 0 if t != 3 else TOKENS - P
             return scores_psum[n][(0, 1, 2, 1)[t]][:, first : first + width]
 
-        def scores(n):
+        def scores(n, tiles):
             g, h = divmod(n, HEADS)
             q_t = qk_turned[n][:, 0, :]
             k_t = qk_turned[n][:, 1, :]
-            scores_psum[n] = [psum_qk.tile([P, TOKENS], F32, name="qk_acc", tag="qk") for bank in range(3)]
-            for t in range(TILES):
+            if 0 in tiles:
+                scores_psum[n] = [psum_qk.tile([P, TOKENS], F32, name="qk_acc", tag="qk") for bank in range(3)]
+            for t in tiles:
                 acc = block(n, t)
                 nc.tensor.matmul(
                     out=acc, lhsT=k_t[:, t * P : (t + 1) * P], rhs=q_t[:, t * P : TOKENS], start=True, stop=False
@@ -298,7 +310,7 @@ def tile_networklayer_pb_t_kernel(tc, q_pos, k_pos, x_grp, Wv, bv, out):
                 )
             row = work[n][:, 2, 2 * P : TOKENS]
             nc.vector.tensor_scalar(out=row, in0=row, scalar1=INV_EPS, scalar2=0.5, op0=ALU.min, op1=ALU.add)
-            for t in (0, 2, 1, 3):
+            for t in (0, 1, 3, 2):
                 row = work[n][:, t, t * P : TOKENS]
                 if t in BY_MATMUL:
                     nc.vector.scalar_tensor_tensor(
@@ -344,7 +356,7 @@ def tile_networklayer_pb_t_kernel(tc, q_pos, k_pos, x_grp, Wv, bv, out):
         def attend(n):
             g, h = divmod(n, HEADS)
             cols = slice(h * P, (h + 1) * P)
-            o_psum[n] = psum_mx.tile([P, TILES, P], F32, name="o_acc", tag="mx")
+            o_psum[n] = psum_mx.tile([P, TILES, P], F32, name="o_acc")
             for u in range(TILES):
                 rows = slice(u * P, (u + 1) * P)
                 nc.tensor.matmul_mx(
@@ -362,9 +374,15 @@ def tile_networklayer_pb_t_kernel(tc, q_pos, k_pos, x_grp, Wv, bv, out):
             cols = slice(h * P, (h + 1) * P)
             if h == 0:
                 o_rows[g] = result.tile([P, TILES, MODEL], F32, name="o_rows")
-            nc.vector.tensor_copy(out=o_rows[g][:, :, cols], in_=o_psum[n][:])
-            if h == HEADS - 1:
-                nc.sync.dma_start(out=out[g].rearrange("(u p) j -> p u j", p=P), in_=o_rows[g][:])
+            if n + SQUARES_AHEAD + 3 < ALL_HEADS:
+                nc.vector.tensor_copy(out=o_rows[g][:, :, cols], in_=o_psum[n][:])
+            else:
+                nc.scalar.copy(out=o_rows[g][:, :, cols], in_=o_psum[n][:])
+            target = out[g].rearrange("(u p) j -> p u j", p=P)
+            if g == GROUPS - 1:
+                nc.sync.dma_start(out=target[:, :, cols], in_=o_rows[g][:, :, cols])
+            elif h == HEADS - 1:
+                nc.sync.dma_start(out=target, in_=o_rows[g][:])
 
         wv_raw = raw.tile([P, TILES, MODEL], BF16, name="x_raw")
         load_qk(0)
@@ -381,47 +399,56 @@ def tile_networklayer_pb_t_kernel(tc, q_pos, k_pos, x_grp, Wv, bv, out):
             return 0 <= n < ALL_HEADS
 
         with tc.manual_schedule():
-            for i in range(-9, ALL_HEADS + 2):
+            for i in range(-SQUARES_AHEAD, ALL_HEADS + 4):
                 if i == -5:
                     wv_grouped = stage.tile([P, TOKENS * PACK], BF16, name="x_grouped", align_bytes=64)
-                    for pair in range(2):
-                        turn_rows(wv_raw, wv_grouped, pair)
-                    for pair in range(2):
-                        turn_x(0, pair)
+                    x_grouped[0] = stage.tile([P, TOKENS * PACK], BF16, name="x_grouped", align_bytes=64)
+                    for rows, grouped in ((wv_raw, wv_grouped), (x_raw[0], x_grouped[0])):
+                        for pair in range(2):
+                            group_rows(turn_rows(rows, pair, psum_qk, "qk"), grouped, pair)
                     quantise(wv_codes[:], wv_scales[:], wv_grouped[:])
                     quantise_x(0)
                     load_x(3)
-                if valid(i - 1):
-                    quantise_w(i - 1)
+                g, h = divmod(i + 3, HEADS)
+                next_x = valid(i + 3) and g + 1 < GROUPS
                 if valid(i + 3):
-                    turn_qk(i + 3)
-                    turn_norms(i + 3)
                     copy_qk(i + 3)
-                    copy_norms(i + 3)
-                if valid(i - 1):
-                    attend(i - 1)
-                    copy_out(i - 1)
+                if next_x and h in (1, 2):
+                    group_x(g + 1, h - 1)
+                if valid(i - 3):
+                    copy_out(i - 3)
+                if valid(i + 2):
+                    add_bias(i + 2)
                 if valid(i + 3):
-                    project(i + 3)
+                    turn_norms(i + 3)
+                if valid(i + 4):
+                    turn_qk(i + 4)
                 if valid(i + 1):
                     inverse_root(i + 1)
+                if valid(i + 2):
+                    scores(i + 2, (0,))
+                if valid(i + 3):
+                    project(i + 3)
+                if valid(i - 2):
+                    attend(i - 2)
+                if valid(i + 2):
+                    scores(i + 2, (1, 3, 2))
+                if valid(i + 3):
+                    copy_norms(i + 3)
+                if next_x and h in (0, 1):
+                    turn_x(g + 1, h)
+                if valid(i - 1):
+                    quantise_w(i - 1)
+                if valid(i + 1):
+                    quantise_v(i + 1)
+                if next_x and h == 3:
+                    quantise_x(g + 1)
                 if valid(i):
                     weigh(i)
                 if (i + 5) % HEADS == 0 and valid(i + 5):
                     split_norms((i + 5) // HEADS)
-                if valid(i + 2):
-                    quantise_v(i + 2)
-                    scores(i + 2)
-                if valid(i + 3):
-                    add_bias(i + 3)
-                    g, h = divmod(i + 3, HEADS)
-                    if g + 1 < GROUPS:
-                        if h in (1, 2):
-                            turn_x(g + 1, h - 1)
-                        if h == 3:
-                            quantise_x(g + 1)
-                            if g + 4 < GROUPS:
-                                load_qk(g + 4)
-                                load_x(g + 4)
-                if valid(i + 9):
-                    square(i + 9)
+                if valid(i + SQUARES_AHEAD):
+                    square(i + SQUARES_AHEAD)
+                if valid(i + 4) and h == 2 and g + 4 < GROUPS:
+                    load_qk(g + 4)
+                    load_x(g + 4)

@@ -22,11 +22,16 @@ EPS = 1.0e-12
 INV_EPS = 1.0e6
 SPLIT = 3
 SLOT = 32
+KEY_ROW = 16
+HEAD_STEP = TILES * P + SLOT
 BY_MATMUL = [0, 1, 3]
 MASKED = -(2.0**95)
 ALL_HEADS = GROUPS * HEADS
 W_BUFS = 3
-SQUARES_AHEAD = 9
+VECTOR_COPIES = ALL_HEADS - 13
+ON_GPSIMD = 6
+RETURNED = (2,)
+FOLDS = 2
 RUN = 4
 
 FLOPS = 3 * 2 * GROUPS * TOKENS * MODEL * MODEL
@@ -39,8 +44,10 @@ def tile_networklayer_pb_t_kernel(tc, q_pos, k_pos, x_grp, Wv, bv, out):
         raw = ctx.enter_context(tc.tile_pool(name="raw", bufs=4))
         stage = ctx.enter_context(tc.tile_pool(name="stage", bufs=2))
         norms = ctx.enter_context(tc.tile_pool(name="norms", bufs=4))
+        fold = ctx.enter_context(tc.tile_pool(name="fold", bufs=5))
         turned = ctx.enter_context(tc.tile_pool(name="turned", bufs=3))
         dist = ctx.enter_context(tc.tile_pool(name="dist", bufs=3))
+        wfirst = ctx.enter_context(tc.tile_pool(name="wfirst", bufs=3))
         wcode = ctx.enter_context(tc.tile_pool(name="wcode", bufs=3))
         vcode = ctx.enter_context(tc.tile_pool(name="vcode", bufs=3))
         result = ctx.enter_context(tc.tile_pool(name="result", bufs=2))
@@ -63,6 +70,20 @@ def tile_networklayer_pb_t_kernel(tc, q_pos, k_pos, x_grp, Wv, bv, out):
             base=0,
             channel_multiplier=1,
         )
+        allowed = const.tile([P, P], BF16, name="allowed")
+        nc.gpsimd.memset(allowed[:], 1.0)
+        nc.gpsimd.affine_select(
+            out=allowed[:],
+            in_=allowed[:],
+            pattern=[[1, P]],
+            compare_op=ALU.is_ge,
+            fill=0.0,
+            base=0,
+            channel_multiplier=-1,
+        )
+        one = const.tile([P, 1], F32, name="one")
+        nc.vector.memset(one[:], 1.0)
+        nc.scalar.activation(out=one[:], in_=one[:], func=ACT.Abs_reciprocal_sqrt)
         bias = const.tile([P, MODEL], BF16, name="bias")
         squares = const.tile([P, 2, 2 * TILES, P], F32, name="squares")
         weights = [
@@ -72,13 +93,22 @@ def tile_networklayer_pb_t_kernel(tc, q_pos, k_pos, x_grp, Wv, bv, out):
         for w_tile in weights:
             nc.vector.memset(w_tile[:], 0.0)
         split_q = [const.tile([P, TILES, P], BF16, name="split_q%d" % i) for i in range(2)]
-        split_k = [const.tile([P, HEADS, TILES, P], BF16, name="split_k%d" % i) for i in range(2)]
+        split_k = [const.tile([P, HEADS * HEAD_STEP], BF16, name="split_k%d" % i) for i in range(2)]
+
+        def query_rows(i, first, heads):
+            rows = split_q[i][:].rearrange("p u (h s) -> p h u s", s=SLOT)
+            return rows[:, heads, :, first : first + SPLIT]
+
+        def key_rows(i, first, heads):
+            rows = split_k[i][:].rearrange("p (h x) -> p h x", x=HEAD_STEP)[:, :, 0 : TILES * P]
+            return rows.rearrange("p h (t c) -> p h t c", c=P)[:, heads, :, first : first + SPLIT]
+
+        all_heads = slice(0, HEADS)
         for i in range(2):
             nc.gpsimd.memset(split_q[i][:], 0.0)
             nc.gpsimd.memset(split_k[i][:], 0.0)
-            for h in range(HEADS):
-                nc.gpsimd.memset(split_q[i][:, :, h * SLOT + SPLIT : h * SLOT + 2 * SPLIT], -0.5)
-                nc.gpsimd.memset(split_k[i][:, h, :, h * SLOT : h * SLOT + SPLIT], -0.5)
+            nc.gpsimd.memset(query_rows(i, KEY_ROW, all_heads), -0.5)
+            nc.gpsimd.memset(key_rows(i, 0, all_heads), -0.5)
         wv_codes = const.tile([P, MODEL], U32, name="wv_codes", align_bytes=64)
         wv_scales = const.tile([P, MODEL], U8, name="wv_scales", align_bytes=64)
 
@@ -97,6 +127,7 @@ def tile_networklayer_pb_t_kernel(tc, q_pos, k_pos, x_grp, Wv, bv, out):
         v_scales = {}
         norm_sums = {}
         half_norms = {}
+        folds = {}
         qk_psum = {}
         qk_turned = {}
         scores_psum = {}
@@ -111,11 +142,17 @@ def tile_networklayer_pb_t_kernel(tc, q_pos, k_pos, x_grp, Wv, bv, out):
             x_raw[g] = raw.tile([P, TILES, MODEL], BF16, name="x_raw")
             nc.sync.dma_start(out=x_raw[g][:], in_=x_grp[g].rearrange("(t p) k -> p t k", p=P))
 
-        def load_qk(g):
-            q_raw[g] = raw.tile([P, HEADS * TILES, P], BF16, name="q_raw")
-            nc.sync.dma_start(out=q_raw[g][:], in_=q_pos[g].rearrange("h (u p) d -> p (h u) d", p=P))
+        def load_qk(g, pieces):
             k_raw[g] = raw.tile([P, HEADS * TILES, P], BF16, name="k_raw")
-            nc.sync.dma_start(out=k_raw[g][:], in_=k_pos[g].rearrange("h (u p) d -> p (h u) d", p=P))
+            q_raw[g] = raw.tile([P, HEADS * TILES, P], BF16, name="q_raw")
+            heads = HEADS // pieces
+            for first in range(0, HEADS, heads):
+                rows = slice(first * TILES, (first + heads) * TILES)
+                for target, source in ((k_raw[g], k_pos[g]), (q_raw[g], q_pos[g])):
+                    nc.sync.dma_start(
+                        out=target[:, rows, :],
+                        in_=source[first : first + heads].rearrange("h (u p) d -> p (h u) d", p=P),
+                    )
 
         def turn_rows(rows, pair, pool, tag):
             words = rows[:].bitcast(F32)
@@ -129,9 +166,9 @@ def tile_networklayer_pb_t_kernel(tc, q_pos, k_pos, x_grp, Wv, bv, out):
                     )
             return tp
 
-        def group_rows(tp, grouped, pair):
+        def group_rows(tp, grouped, pair, copy):
             grouped_words = grouped[:].bitcast(F32).rearrange("p (r u) -> p r u", u=2)
-            nc.vector.tensor_copy(
+            copy(
                 out=grouped_words[:, 2 * pair * P : 2 * (pair + 1) * P, :],
                 in_=tp[:].rearrange("p u r -> p r u"),
             )
@@ -145,7 +182,7 @@ def tile_networklayer_pb_t_kernel(tc, q_pos, k_pos, x_grp, Wv, bv, out):
         def group_x(g, pair):
             if pair == 0:
                 x_grouped[g] = stage.tile([P, TOKENS * PACK], BF16, name="x_grouped", align_bytes=64)
-            group_rows(x_psum[g], x_grouped[g], pair)
+            group_rows(x_psum[g], x_grouped[g], pair, nc.scalar.copy)
 
         def quantise_x(g):
             x_codes[g] = stage.tile([P, TOKENS], U32, name="x_codes", align_bytes=64)
@@ -157,45 +194,67 @@ def tile_networklayer_pb_t_kernel(tc, q_pos, k_pos, x_grp, Wv, bv, out):
             if h == 0:
                 norm_sums[g] = norms.tile([P, HEADS, 2, TILES], F32, name="norm_sums")
             for i, source in enumerate((q_raw[g], k_raw[g])):
+                if i == 0 and n >= ON_GPSIMD:
+                    continue
                 for u in range(TILES):
                     rows = source[:, h * TILES + u, :]
                     unused = squares[:, n % 2, i * TILES + u, :]
                     total = norm_sums[g][:, h, i, u : u + 1]
-                    if g == 0 and i == 0:
+                    if i == 0 and h < 2:
                         nc.vector.scalar_tensor_tensor(
                             out=unused, in0=rows, scalar=1.0, in1=rows, op0=ALU.mult, op1=ALU.mult, accum_out=total
                         )
                     else:
                         nc.scalar.activation(out=unused, in_=rows, func=ACT.Square, accum_out=total)
+            if n >= ON_GPSIMD:
+                rows = q_raw[g][:, h * TILES : (h + 1) * TILES, :]
+                folds[n] = [fold.tile([P, TILES, P >> i], F32, name="fold%d" % i) for i in range(FOLDS + 1)]
+                for u in (0, 2):
+                    nc.gpsimd.tensor_tensor(
+                        out=folds[n][0][:, u : u + 2, :], in0=rows[:, u : u + 2, :], in1=rows[:, u : u + 2, :], op=ALU.mult
+                    )
+                for i in range(FOLDS):
+                    half = P >> (i + 1)
+                    nc.gpsimd.tensor_tensor(
+                        out=folds[n][i + 1][:],
+                        in0=folds[n][i][:, :, 0:half],
+                        in1=folds[n][i][:, :, half : 2 * half],
+                        op=ALU.add,
+                    )
 
-        def split_norms(g):
-            sums = norm_sums[g]
-            half_norms[g] = norms.tile([P, HEADS, 2, TILES], F32, name="half_norms")
-            nc.gpsimd.tensor_scalar(
-                out=half_norms[g][:], in0=sums[:], scalar1=-0.5, scalar2=0.0, op0=ALU.mult, op1=ALU.add
-            )
+        def sum_folds(n):
+            g, h = divmod(n, HEADS)
+            if n >= ON_GPSIMD:
+                nc.vector.tensor_reduce(
+                    out=norm_sums[g][:, h, 0, :], in_=folds[n][FOLDS][:], axis=mybir.AxisListType.X, op=ALU.add
+                )
+
+        def split_norms(g, heads, engine):
+            if heads.start == 0:
+                half_norms[g] = norms.tile([P, HEADS, 2, TILES], F32, name="half_norms")
+            sums = norm_sums[g][:, heads]
             terms = norms.tile([P, SPLIT, HEADS, 2, TILES], BF16, name="terms")
-            rest = norms.tile([P, HEADS, 2, TILES], F32, name="rest")
-            nc.gpsimd.tensor_copy(out=terms[:, 0], in_=sums[:])
-            nc.gpsimd.tensor_tensor(out=rest[:], in0=sums[:], in1=terms[:, 0], op=ALU.subtract)
-            nc.gpsimd.tensor_copy(out=terms[:, 1], in_=rest[:])
-            nc.gpsimd.tensor_tensor(out=terms[:, 2], in0=rest[:], in1=terms[:, 1], op=ALU.subtract)
-            for h in range(HEADS):
-                nc.gpsimd.tensor_copy(
-                    out=split_q[g % 2][:, :, h * SLOT : h * SLOT + SPLIT],
-                    in_=terms[:, :, h, 0, :].rearrange("p i u -> p u i"),
-                )
-                nc.gpsimd.tensor_copy(
-                    out=split_k[g % 2][:, h, :, h * SLOT + SPLIT : h * SLOT + 2 * SPLIT],
-                    in_=terms[:, :, h, 1, :].rearrange("p i u -> p u i"),
-                )
+            rest = norms.tile([P, HEADS, 2, TILES], F32, name="rest")[:, heads]
+            engine.tensor_copy(out=terms[:, 0, heads], in_=sums)
+            engine.tensor_tensor(out=rest, in0=sums, in1=terms[:, 0, heads], op=ALU.subtract)
+            engine.tensor_copy(out=terms[:, 1, heads], in_=rest)
+            engine.tensor_tensor(out=terms[:, 2, heads], in0=rest, in1=terms[:, 1, heads], op=ALU.subtract)
+            for side, rows in ((0, query_rows(g % 2, 0, heads)), (1, key_rows(g % 2, KEY_ROW, heads))):
+                engine.tensor_copy(out=rows, in_=terms[:, :, heads, side, :].rearrange("p i h u -> p h u i"))
+            engine.tensor_scalar(
+                out=half_norms[g][:, heads], in0=sums, scalar1=-0.5, scalar2=0.0, op0=ALU.mult, op1=ALU.add
+            )
 
         def turn_norms(n):
             g, h = divmod(n, HEADS)
             norm_psum[n] = psum_tp.tile([P, 2, TILES, P], BF16, name="tp_norms", tag="tp_side")
             for slot, t in enumerate(BY_MATMUL):
-                nc.tensor.transpose(out=norm_psum[n][:, 0, slot, :], in_=split_k[g % 2][:, h, t, :], identity=ident_b[:])
-            if h == 0:
+                nc.tensor.transpose(
+                    out=norm_psum[n][:, 0, slot, :],
+                    in_=split_k[g % 2][:, (h * TILES + t) * P : (h * TILES + t + 1) * P],
+                    identity=ident_b[:],
+                )
+            if h == 0 or n in RETURNED:
                 for u in range(TILES):
                     nc.tensor.transpose(out=norm_psum[n][:, 1, u, :], in_=split_q[g % 2][:, u, :], identity=ident_b[:])
 
@@ -203,18 +262,19 @@ def tile_networklayer_pb_t_kernel(tc, q_pos, k_pos, x_grp, Wv, bv, out):
             g, h = divmod(n, HEADS)
             slots = len(BY_MATMUL)
             k_side[n] = turned.tile([P, slots, P], BF16, name="k_side")
-            nc.vector.tensor_copy(out=k_side[n][:], in_=norm_psum[n][:, 0, 0:slots, :])
-            if h == 0:
+            nc.scalar.copy(out=k_side[n][:], in_=norm_psum[n][:, 0, 0:slots, :])
+            if h == 0 or n in RETURNED:
                 q_side[g] = turned.tile([P, TOKENS], BF16, name="q_side")
-                nc.vector.tensor_copy(
+                nc.scalar.copy(
                     out=q_side[g][:], in_=norm_psum[n][:, 1].rearrange("p u b -> p (u b)")
                 )
 
-        def turn_qk(n):
+        def turn_qk(n, tiles):
             g, h = divmod(n, HEADS)
-            qk_psum[n] = psum_tp.tile([P, 2 * TILES, P], BF16, name="tp_qk", tag="tp_qk")
+            if 0 in tiles:
+                qk_psum[n] = psum_tp.tile([P, 2 * TILES, P], BF16, name="tp_qk", tag="tp_qk")
             for i, source in enumerate((q_raw[g], k_raw[g])):
-                for u in range(TILES):
+                for u in tiles:
                     nc.tensor.transpose(
                         out=qk_psum[n][:, i * TILES + u, :],
                         in_=source[:, h * TILES + u, :],
@@ -279,9 +339,10 @@ def tile_networklayer_pb_t_kernel(tc, q_pos, k_pos, x_grp, Wv, bv, out):
                 nc.tensor.matmul(
                     out=acc, lhsT=k_t[:, t * P : (t + 1) * P], rhs=q_t[:, t * P : TOKENS], start=True, stop=False
                 )
-                nc.tensor.matmul(
-                    out=acc[:, 0:P], lhsT=mask[:], rhs=ident_f[:], is_transpose=True, start=False, stop=False
-                )
+                if t > 0:
+                    nc.tensor.matmul(
+                        out=acc[:, 0:P], lhsT=mask[:], rhs=ident_f[:], is_transpose=True, start=False, stop=False
+                    )
                 if t in BY_MATMUL:
                     nc.tensor.matmul(
                         out=acc, lhsT=k_side[n][:, BY_MATMUL.index(t), :], rhs=q_side[g][:, t * P : TOKENS], start=False, stop=True
@@ -328,7 +389,11 @@ def tile_networklayer_pb_t_kernel(tc, q_pos, k_pos, x_grp, Wv, bv, out):
 
         def weigh(n):
             w_tile = weights[n % W_BUFS]
-            for u in range(TILES):
+            first = wfirst.tile([P, P], BF16, name="first")
+            nc.scalar.activation(
+                out=first[:], in_=work[n][:, 0, 0:P], func=ACT.Abs_reciprocal_sqrt, scale=-4.0, bias=1.0
+            )
+            for u in range(1, TILES):
                 cols = slice(u * P, (u + 1) * P)
                 nc.scalar.activation(
                     out=w_tile[:, cols, 0 : u + 1].rearrange("p (c i) t -> p c t i", i=RUN),
@@ -337,16 +402,7 @@ def tile_networklayer_pb_t_kernel(tc, q_pos, k_pos, x_grp, Wv, bv, out):
                     scale=-4.0,
                     bias=1.0,
                 )
-            first = w_tile[:, 0:P, 0]
-            nc.gpsimd.affine_select(
-                out=first,
-                in_=first,
-                pattern=[[1, P]],
-                compare_op=ALU.is_ge,
-                fill=0.0,
-                base=0,
-                channel_multiplier=-1,
-            )
+            nc.gpsimd.tensor_tensor(out=w_tile[:, 0:P, 0], in0=first[:], in1=allowed[:], op=ALU.mult)
 
         def quantise_w(n):
             w_codes[n] = wcode.tile([P, TOKENS], U32, name="w_codes", align_bytes=64)
@@ -374,7 +430,7 @@ def tile_networklayer_pb_t_kernel(tc, q_pos, k_pos, x_grp, Wv, bv, out):
             cols = slice(h * P, (h + 1) * P)
             if h == 0:
                 o_rows[g] = result.tile([P, TILES, MODEL], F32, name="o_rows")
-            if n + SQUARES_AHEAD + 3 < ALL_HEADS:
+            if n < VECTOR_COPIES:
                 nc.vector.tensor_copy(out=o_rows[g][:, :, cols], in_=o_psum[n][:])
             else:
                 nc.scalar.copy(out=o_rows[g][:, :, cols], in_=o_psum[n][:])
@@ -385,70 +441,95 @@ def tile_networklayer_pb_t_kernel(tc, q_pos, k_pos, x_grp, Wv, bv, out):
                 nc.sync.dma_start(out=target, in_=o_rows[g][:])
 
         wv_raw = raw.tile([P, TILES, MODEL], BF16, name="x_raw")
-        load_qk(0)
+        load_qk(0, 2)
         nc.sync.dma_start(out=wv_raw[:], in_=Wv.rearrange("(t p) k -> p t k", p=P))
         load_x(0)
+        load_qk(1, 1)
         nc.sync.dma_start(out=bias[:], in_=bv.partition_broadcast(P))
-        load_qk(1)
         load_x(1)
-        load_qk(2)
+        load_qk(2, 1)
         load_x(2)
-        load_qk(3)
+        load_qk(3, 1)
 
         def valid(n):
             return 0 <= n < ALL_HEADS
 
+        def square_step(n):
+            return -1 if n < 2 * HEADS else max(n - 11, n // 2 - 4)
+
+        def sum_step(n):
+            return max(n - 8, n // 2 - 2)
+
         with tc.manual_schedule():
-            for i in range(-SQUARES_AHEAD, ALL_HEADS + 4):
-                if i == -5:
+            for n in range(HEADS // 2):
+                square(n)
+            split_norms(0, slice(0, HEADS // 2), nc.vector)
+            for i in range(-4, ALL_HEADS + 4):
+                g, h = divmod(i + 3, HEADS)
+                next_x = valid(i + 3) and g + 1 < GROUPS
+                if i == 0:
+                    for n in range(ON_GPSIMD, 2 * HEADS):
+                        sum_folds(n)
+                    split_norms(1, all_heads, nc.gpsimd)
+                if next_x and h in (2, 3):
+                    group_x(g + 1, h - 2)
+                if valid(i - 3):
+                    copy_out(i - 3)
+                if valid(i + 1):
+                    add_bias(i + 1)
+                if valid(i + 3):
+                    copy_qk(i + 3)
+                if i == -3:
+                    for n in range(HEADS // 2, HEADS):
+                        square(n)
                     wv_grouped = stage.tile([P, TOKENS * PACK], BF16, name="x_grouped", align_bytes=64)
                     x_grouped[0] = stage.tile([P, TOKENS * PACK], BF16, name="x_grouped", align_bytes=64)
-                    for rows, grouped in ((wv_raw, wv_grouped), (x_raw[0], x_grouped[0])):
+                    for rows, grouped, copy in (
+                        (wv_raw, wv_grouped, nc.scalar.copy),
+                        (x_raw[0], x_grouped[0], nc.vector.tensor_copy),
+                    ):
                         for pair in range(2):
-                            group_rows(turn_rows(rows, pair, psum_qk, "qk"), grouped, pair)
+                            group_rows(turn_rows(rows, pair, psum_qk, "qk"), grouped, pair, copy)
                     quantise(wv_codes[:], wv_scales[:], wv_grouped[:])
                     quantise_x(0)
                     load_x(3)
-                g, h = divmod(i + 3, HEADS)
-                next_x = valid(i + 3) and g + 1 < GROUPS
-                if valid(i + 3):
-                    copy_qk(i + 3)
-                if next_x and h in (1, 2):
-                    group_x(g + 1, h - 1)
-                if valid(i - 3):
-                    copy_out(i - 3)
-                if valid(i + 2):
-                    add_bias(i + 2)
                 if valid(i + 3):
                     turn_norms(i + 3)
-                if valid(i + 4):
-                    turn_qk(i + 4)
                 if valid(i + 1):
                     inverse_root(i + 1)
-                if valid(i + 2):
-                    scores(i + 2, (0,))
-                if valid(i + 3):
-                    project(i + 3)
-                if valid(i - 2):
-                    attend(i - 2)
-                if valid(i + 2):
-                    scores(i + 2, (1, 3, 2))
                 if valid(i + 3):
                     copy_norms(i + 3)
-                if next_x and h in (0, 1):
-                    turn_x(g + 1, h)
+                if i == -3:
+                    split_norms(0, slice(HEADS // 2, HEADS), nc.gpsimd)
+                if valid(i + 2):
+                    scores(i + 2, (0,))
+                if valid(i + 2):
+                    project(i + 2)
+                if valid(i - 2):
+                    attend(i - 2)
+                for t, turned_tiles in ((1, (0, 1)), (3, (2,)), (2, (3,))):
+                    if valid(i + 2):
+                        scores(i + 2, (t,))
+                    if valid(i + 4):
+                        turn_qk(i + 4, turned_tiles)
+                if next_x and h in (1, 2):
+                    turn_x(g + 1, h - 1)
                 if valid(i - 1):
                     quantise_w(i - 1)
-                if valid(i + 1):
-                    quantise_v(i + 1)
+                if valid(i):
+                    quantise_v(i)
                 if next_x and h == 3:
                     quantise_x(g + 1)
                 if valid(i):
                     weigh(i)
-                if (i + 5) % HEADS == 0 and valid(i + 5):
-                    split_norms((i + 5) // HEADS)
-                if valid(i + SQUARES_AHEAD):
-                    square(i + SQUARES_AHEAD)
+                for n in range(2 * HEADS, ALL_HEADS):
+                    if sum_step(n) == i:
+                        sum_folds(n)
+                if (i + 5) % HEADS == 0 and 2 * HEADS <= i + 5 < ALL_HEADS:
+                    split_norms((i + 5) // HEADS, all_heads, nc.gpsimd)
+                for n in range(HEADS, ALL_HEADS):
+                    if square_step(n) == i:
+                        square(n)
                 if valid(i + 4) and h == 2 and g + 4 < GROUPS:
-                    load_qk(g + 4)
+                    load_qk(g + 4, 1)
                     load_x(g + 4)

@@ -29,7 +29,7 @@ MASKED = -(2.0**95)
 ALL_HEADS = GROUPS * HEADS
 W_BUFS = 3
 VECTOR_COPIES = ALL_HEADS - 13
-ON_GPSIMD = 6
+ON_GPSIMD = 8
 RETURNED = (2,)
 FOLDS = 2
 RUN = 4
@@ -44,7 +44,7 @@ def tile_networklayer_pb_t_kernel(tc, q_pos, k_pos, x_grp, Wv, bv, out):
         raw = ctx.enter_context(tc.tile_pool(name="raw", bufs=4))
         stage = ctx.enter_context(tc.tile_pool(name="stage", bufs=2))
         norms = ctx.enter_context(tc.tile_pool(name="norms", bufs=4))
-        fold = ctx.enter_context(tc.tile_pool(name="fold", bufs=5))
+        fold = ctx.enter_context(tc.tile_pool(name="fold", bufs=1))
         turned = ctx.enter_context(tc.tile_pool(name="turned", bufs=3))
         dist = ctx.enter_context(tc.tile_pool(name="dist", bufs=3))
         wfirst = ctx.enter_context(tc.tile_pool(name="wfirst", bufs=3))
@@ -361,7 +361,7 @@ def tile_networklayer_pb_t_kernel(tc, q_pos, k_pos, x_grp, Wv, bv, out):
         def inverse_root(n):
             g, h = divmod(n, HEADS)
             work[n] = dist.tile([P, TILES, TOKENS], F32, name="work")
-            for t in (2, 0, 1, 3):
+            for t in (0, 1, 3, 2):
                 nc.scalar.activation(
                     out=work[n][:, t, t * P : TOKENS],
                     in_=block(n, t),
@@ -369,23 +369,27 @@ def tile_networklayer_pb_t_kernel(tc, q_pos, k_pos, x_grp, Wv, bv, out):
                     scale=-2.0,
                     bias=EPS if t in BY_MATMUL else norm_sums[g][:, h, 1, t : t + 1],
                 )
+
+        def expand(n):
+            for t in BY_MATMUL:
+                row = work[n][:, t, t * P : TOKENS]
+                nc.vector.scalar_tensor_tensor(
+                    out=row, in0=row, scalar=0.5, in1=block(n, t), op0=ALU.add, op1=ALU.mult
+                )
             row = work[n][:, 2, 2 * P : TOKENS]
             nc.vector.tensor_scalar(out=row, in0=row, scalar1=INV_EPS, scalar2=0.5, op0=ALU.min, op1=ALU.add)
-            for t in (0, 1, 3, 2):
-                row = work[n][:, t, t * P : TOKENS]
-                if t in BY_MATMUL:
-                    nc.vector.scalar_tensor_tensor(
-                        out=row, in0=row, scalar=0.5, in1=block(n, t), op0=ALU.add, op1=ALU.mult
-                    )
-                else:
-                    nc.vector.scalar_tensor_tensor(
-                        out=row,
-                        in0=block(n, t),
-                        scalar=half_norms[g][:, h, 1, t : t + 1],
-                        in1=row,
-                        op0=ALU.add,
-                        op1=ALU.mult,
-                    )
+
+        def expand_last(n):
+            g, h = divmod(n, HEADS)
+            row = work[n][:, 2, 2 * P : TOKENS]
+            nc.vector.scalar_tensor_tensor(
+                out=row,
+                in0=block(n, 2),
+                scalar=half_norms[g][:, h, 1, 2:3],
+                in1=row,
+                op0=ALU.add,
+                op1=ALU.mult,
+            )
 
         def weigh(n):
             w_tile = weights[n % W_BUFS]
@@ -454,12 +458,6 @@ def tile_networklayer_pb_t_kernel(tc, q_pos, k_pos, x_grp, Wv, bv, out):
         def valid(n):
             return 0 <= n < ALL_HEADS
 
-        def square_step(n):
-            return -1 if n < 2 * HEADS else max(n - 11, n // 2 - 4)
-
-        def sum_step(n):
-            return max(n - 8, n // 2 - 2)
-
         with tc.manual_schedule():
             for n in range(HEADS // 2):
                 square(n)
@@ -467,10 +465,6 @@ def tile_networklayer_pb_t_kernel(tc, q_pos, k_pos, x_grp, Wv, bv, out):
             for i in range(-4, ALL_HEADS + 4):
                 g, h = divmod(i + 3, HEADS)
                 next_x = valid(i + 3) and g + 1 < GROUPS
-                if i == 0:
-                    for n in range(ON_GPSIMD, 2 * HEADS):
-                        sum_folds(n)
-                    split_norms(1, all_heads, nc.gpsimd)
                 if next_x and h in (2, 3):
                     group_x(g + 1, h - 2)
                 if valid(i - 3):
@@ -497,6 +491,7 @@ def tile_networklayer_pb_t_kernel(tc, q_pos, k_pos, x_grp, Wv, bv, out):
                     turn_norms(i + 3)
                 if valid(i + 1):
                     inverse_root(i + 1)
+                    expand(i + 1)
                 if valid(i + 3):
                     copy_norms(i + 3)
                 if i == -3:
@@ -516,20 +511,23 @@ def tile_networklayer_pb_t_kernel(tc, q_pos, k_pos, x_grp, Wv, bv, out):
                     turn_x(g + 1, h - 1)
                 if valid(i - 1):
                     quantise_w(i - 1)
+                if valid(i + 1):
+                    expand_last(i + 1)
                 if valid(i):
                     quantise_v(i)
                 if next_x and h == 3:
                     quantise_x(g + 1)
                 if valid(i):
                     weigh(i)
-                for n in range(2 * HEADS, ALL_HEADS):
-                    if sum_step(n) == i:
-                        sum_folds(n)
-                if (i + 5) % HEADS == 0 and 2 * HEADS <= i + 5 < ALL_HEADS:
-                    split_norms((i + 5) // HEADS, all_heads, nc.gpsimd)
-                for n in range(HEADS, ALL_HEADS):
-                    if square_step(n) == i:
+                if i == -1:
+                    for n in range(HEADS, ON_GPSIMD):
                         square(n)
+                if ON_GPSIMD <= i + 8 < ALL_HEADS:
+                    sum_folds(i + 8)
+                if ON_GPSIMD <= i + 9 < ALL_HEADS:
+                    square(i + 9)
+                if (i + 5) % HEADS == 0 and HEADS <= i + 5 < ALL_HEADS:
+                    split_norms((i + 5) // HEADS, all_heads, nc.gpsimd)
                 if valid(i + 4) and h == 2 and g + 4 < GROUPS:
                     load_qk(g + 4, 1)
                     load_x(g + 4)

@@ -31,7 +31,8 @@ W_BUFS = 3
 VECTOR_COPIES = ALL_HEADS - 13
 ON_GPSIMD = 8
 RETURNED = (2,)
-FOLDS = 2
+FOLDS = 1
+GPSIMD_TILES = 4
 RUN = 4
 
 FLOPS = 3 * 2 * GROUPS * TOKENS * MODEL * MODEL
@@ -45,7 +46,7 @@ def tile_networklayer_pb_t_kernel(tc, q_pos, k_pos, x_grp, Wv, bv, out):
         stage = ctx.enter_context(tc.tile_pool(name="stage", bufs=2))
         norms = ctx.enter_context(tc.tile_pool(name="norms", bufs=4))
         fold = ctx.enter_context(tc.tile_pool(name="fold", bufs=1))
-        turned = ctx.enter_context(tc.tile_pool(name="turned", bufs=3))
+        turned = ctx.enter_context(tc.tile_pool(name="turned", bufs=4))
         dist = ctx.enter_context(tc.tile_pool(name="dist", bufs=3))
         wfirst = ctx.enter_context(tc.tile_pool(name="wfirst", bufs=3))
         wcode = ctx.enter_context(tc.tile_pool(name="wcode", bufs=3))
@@ -85,13 +86,11 @@ def tile_networklayer_pb_t_kernel(tc, q_pos, k_pos, x_grp, Wv, bv, out):
         nc.vector.memset(one[:], 1.0)
         nc.scalar.activation(out=one[:], in_=one[:], func=ACT.Abs_reciprocal_sqrt)
         bias = const.tile([P, MODEL], BF16, name="bias")
-        squares = const.tile([P, 2, 2 * TILES, P], F32, name="squares")
+        squares = const.tile([P, HEADS, 2 * TILES, P], F32, name="squares")
         weights = [
             const.tile([P, TOKENS, PACK], BF16, name="weights%d" % i, align_bytes=64)
             for i in range(W_BUFS)
         ]
-        for w_tile in weights:
-            nc.vector.memset(w_tile[:], 0.0)
         split_q = [const.tile([P, TILES, P], BF16, name="split_q%d" % i) for i in range(2)]
         split_k = [const.tile([P, HEADS * HEAD_STEP], BF16, name="split_k%d" % i) for i in range(2)]
 
@@ -105,10 +104,10 @@ def tile_networklayer_pb_t_kernel(tc, q_pos, k_pos, x_grp, Wv, bv, out):
 
         all_heads = slice(0, HEADS)
         for i in range(2):
-            nc.gpsimd.memset(split_q[i][:], 0.0)
-            nc.gpsimd.memset(split_k[i][:], 0.0)
-            nc.gpsimd.memset(query_rows(i, KEY_ROW, all_heads), -0.5)
-            nc.gpsimd.memset(key_rows(i, 0, all_heads), -0.5)
+            nc.vector.memset(split_q[i][:].rearrange("p u c -> p (u c)").bitcast(U32), 0)
+            nc.vector.memset(split_k[i][:].bitcast(U32), 0)
+            nc.vector.memset(query_rows(i, KEY_ROW, all_heads), -0.5)
+            nc.vector.memset(key_rows(i, 0, all_heads), -0.5)
         wv_codes = const.tile([P, MODEL], U32, name="wv_codes", align_bytes=64)
         wv_scales = const.tile([P, MODEL], U8, name="wv_scales", align_bytes=64)
 
@@ -182,7 +181,7 @@ def tile_networklayer_pb_t_kernel(tc, q_pos, k_pos, x_grp, Wv, bv, out):
         def group_x(g, pair):
             if pair == 0:
                 x_grouped[g] = stage.tile([P, TOKENS * PACK], BF16, name="x_grouped", align_bytes=64)
-            group_rows(x_psum[g], x_grouped[g], pair, nc.scalar.copy)
+            group_rows(x_psum[g], x_grouped[g], pair, nc.vector.tensor_copy)
 
         def quantise_x(g):
             x_codes[g] = stage.tile([P, TOKENS], U32, name="x_codes", align_bytes=64)
@@ -193,57 +192,64 @@ def tile_networklayer_pb_t_kernel(tc, q_pos, k_pos, x_grp, Wv, bv, out):
             g, h = divmod(n, HEADS)
             if h == 0:
                 norm_sums[g] = norms.tile([P, HEADS, 2, TILES], F32, name="norm_sums")
-            for i, source in enumerate((q_raw[g], k_raw[g])):
-                if i == 0 and n >= ON_GPSIMD:
-                    continue
+            for side, source in ((1, k_raw[g]), (0, q_raw[g])):
                 for u in range(TILES):
                     rows = source[:, h * TILES + u, :]
-                    unused = squares[:, n % 2, i * TILES + u, :]
-                    total = norm_sums[g][:, h, i, u : u + 1]
-                    if i == 0 and h < 2:
+                    unused = squares[:, h, side * TILES + u, :]
+                    total = norm_sums[g][:, h, side, u : u + 1]
+                    if n >= ON_GPSIMD and side * TILES + u < GPSIMD_TILES:
+                        continue
+                    if side == 0 and h < 2:
                         nc.vector.scalar_tensor_tensor(
                             out=unused, in0=rows, scalar=1.0, in1=rows, op0=ALU.mult, op1=ALU.mult, accum_out=total
                         )
                     else:
                         nc.scalar.activation(out=unused, in_=rows, func=ACT.Square, accum_out=total)
-            if n >= ON_GPSIMD:
-                rows = q_raw[g][:, h * TILES : (h + 1) * TILES, :]
-                folds[n] = [fold.tile([P, TILES, P >> i], F32, name="fold%d" % i) for i in range(FOLDS + 1)]
-                for u in (0, 2):
-                    nc.gpsimd.tensor_tensor(
-                        out=folds[n][0][:, u : u + 2, :], in0=rows[:, u : u + 2, :], in1=rows[:, u : u + 2, :], op=ALU.mult
-                    )
-                for i in range(FOLDS):
-                    half = P >> (i + 1)
-                    nc.gpsimd.tensor_tensor(
-                        out=folds[n][i + 1][:],
-                        in0=folds[n][i][:, :, 0:half],
-                        in1=folds[n][i][:, :, half : 2 * half],
-                        op=ALU.add,
-                    )
+
+        def fold_squares(n):
+            g, h = divmod(n, HEADS)
+            folds[n] = [fold.tile([P, GPSIMD_TILES, P >> i], F32, name="fold%d" % i) for i in range(FOLDS + 1)]
+            first = h * TILES
+            for source, start, stop in ((q_raw[g], 0, 2), (q_raw[g], 2, 4), (k_raw[g], 4, GPSIMD_TILES)):
+                if stop > start:
+                    rows = source[:, first + start % TILES : first + start % TILES + stop - start, :]
+                    nc.gpsimd.tensor_tensor(out=folds[n][0][:, start:stop, :], in0=rows, in1=rows, op=ALU.mult)
+            for i in range(FOLDS):
+                half = P >> (i + 1)
+                nc.gpsimd.tensor_tensor(
+                    out=folds[n][i + 1][:],
+                    in0=folds[n][i][:, :, 0:half],
+                    in1=folds[n][i][:, :, half : 2 * half],
+                    op=ALU.add,
+                )
 
         def sum_folds(n):
             g, h = divmod(n, HEADS)
-            if n >= ON_GPSIMD:
-                nc.vector.tensor_reduce(
-                    out=norm_sums[g][:, h, 0, :], in_=folds[n][FOLDS][:], axis=mybir.AxisListType.X, op=ALU.add
-                )
+            sums = norm_sums[g][:, h].rearrange("p i u -> p (i u)")
+            nc.vector.tensor_reduce(
+                out=sums[:, 0:GPSIMD_TILES], in_=folds[n][FOLDS][:], axis=mybir.AxisListType.X, op=ALU.add
+            )
 
-        def split_norms(g, heads, engine):
+        def split_steps(g, heads):
             if heads.start == 0:
                 half_norms[g] = norms.tile([P, HEADS, 2, TILES], F32, name="half_norms")
             sums = norm_sums[g][:, heads]
-            terms = norms.tile([P, SPLIT, HEADS, 2, TILES], BF16, name="terms")
+            all_terms = norms.tile([P, SPLIT, HEADS, 2, TILES], BF16, name="terms")
+            terms = [all_terms[:, i, heads] for i in range(SPLIT)]
             rest = norms.tile([P, HEADS, 2, TILES], F32, name="rest")[:, heads]
-            engine.tensor_copy(out=terms[:, 0, heads], in_=sums)
-            engine.tensor_tensor(out=rest, in0=sums, in1=terms[:, 0, heads], op=ALU.subtract)
-            engine.tensor_copy(out=terms[:, 1, heads], in_=rest)
-            engine.tensor_tensor(out=terms[:, 2, heads], in0=rest, in1=terms[:, 1, heads], op=ALU.subtract)
-            for side, rows in ((0, query_rows(g % 2, 0, heads)), (1, key_rows(g % 2, KEY_ROW, heads))):
-                engine.tensor_copy(out=rows, in_=terms[:, :, heads, side, :].rearrange("p i h u -> p h u i"))
-            engine.tensor_scalar(
-                out=half_norms[g][:, heads], in0=sums, scalar1=-0.5, scalar2=0.0, op0=ALU.mult, op1=ALU.add
-            )
+
+            def place(side, rows):
+                nc.vector.tensor_copy(out=rows, in_=all_terms[:, :, heads, side, :].rearrange("p i h u -> p h u i"))
+
+            return [
+                lambda: nc.vector.tensor_copy(out=terms[0], in_=sums),
+                lambda: nc.vector.tensor_tensor(out=rest, in0=sums, in1=terms[0], op=ALU.subtract),
+                lambda: nc.vector.tensor_copy(out=terms[1], in_=rest),
+                lambda: nc.vector.tensor_tensor(out=terms[2], in0=rest, in1=terms[1], op=ALU.subtract),
+                lambda: place(0, query_rows(g % 2, 0, heads)),
+                lambda: place(1, key_rows(g % 2, KEY_ROW, heads)),
+                lambda: nc.vector.tensor_scalar_mul(out=half_norms[g][:, heads], in0=sums, scalar1=-0.5),
+            ]
 
         def turn_norms(n):
             g, h = divmod(n, HEADS)
@@ -434,7 +440,7 @@ def tile_networklayer_pb_t_kernel(tc, q_pos, k_pos, x_grp, Wv, bv, out):
             cols = slice(h * P, (h + 1) * P)
             if h == 0:
                 o_rows[g] = result.tile([P, TILES, MODEL], F32, name="o_rows")
-            if n < VECTOR_COPIES:
+            if n < VECTOR_COPIES and h == 0:
                 nc.vector.tensor_copy(out=o_rows[g][:, :, cols], in_=o_psum[n][:])
             else:
                 nc.scalar.copy(out=o_rows[g][:, :, cols], in_=o_psum[n][:])
@@ -446,14 +452,14 @@ def tile_networklayer_pb_t_kernel(tc, q_pos, k_pos, x_grp, Wv, bv, out):
 
         wv_raw = raw.tile([P, TILES, MODEL], BF16, name="x_raw")
         load_qk(0, 2)
+        load_qk(1, 1)
         nc.sync.dma_start(out=wv_raw[:], in_=Wv.rearrange("(t p) k -> p t k", p=P))
         load_x(0)
-        load_qk(1, 1)
         nc.sync.dma_start(out=bias[:], in_=bv.partition_broadcast(P))
-        load_x(1)
         load_qk(2, 1)
-        load_x(2)
+        load_x(1)
         load_qk(3, 1)
+        load_x(2)
 
         def valid(n):
             return 0 <= n < ALL_HEADS
@@ -461,73 +467,90 @@ def tile_networklayer_pb_t_kernel(tc, q_pos, k_pos, x_grp, Wv, bv, out):
         with tc.manual_schedule():
             for n in range(HEADS // 2):
                 square(n)
-            split_norms(0, slice(0, HEADS // 2), nc.vector)
+            for step in split_steps(0, slice(0, HEADS // 2)):
+                step()
             for i in range(-4, ALL_HEADS + 4):
                 g, h = divmod(i + 3, HEADS)
-                next_x = valid(i + 3) and g + 1 < GROUPS
-                if next_x and h in (2, 3):
-                    group_x(g + 1, h - 2)
+                steps = []
+                if (i + 5) % HEADS == 0 and 2 * HEADS <= i + 5 < ALL_HEADS:
+                    steps = split_steps((i + 5) // HEADS, all_heads)
+                steps = steps + [lambda: None] * (7 - len(steps))
                 if valid(i - 3):
                     copy_out(i - 3)
-                if valid(i + 1):
-                    add_bias(i + 1)
+                if valid(i - 1):
+                    add_bias(i - 1)
                 if valid(i + 3):
                     copy_qk(i + 3)
                 if i == -3:
                     for n in range(HEADS // 2, HEADS):
                         square(n)
+                    for step in split_steps(0, slice(HEADS // 2, HEADS)):
+                        step()
+                    for w_tile in weights:
+                        nc.vector.memset(w_tile[:].rearrange("p b t -> p (b t)").bitcast(U32), 0)
+                if valid(i + 1):
+                    inverse_root(i + 1)
+                if valid(i + 1):
+                    expand(i + 1)
+                if valid(i + 3):
+                    copy_norms(i + 3)
+                if valid(i + 2):
+                    scores(i + 2, (0,))
+                if h in (0, 1) and 0 < g < GROUPS:
+                    turn_x(g, h)
+                if valid(i):
+                    project(i)
+                if valid(i - 2):
+                    attend(i - 2)
+                if valid(i + 2):
+                    scores(i + 2, (1,))
+                if valid(i + 2):
+                    scores(i + 2, (3,))
+                if valid(i + 2):
+                    scores(i + 2, (2,))
+                if valid(i + 4):
+                    turn_qk(i + 4, range(TILES))
+                if valid(i - 1):
+                    quantise_w(i - 1)
+                steps[0]()
+                if valid(i + 1):
+                    expand_last(i + 1)
+                steps[1]()
+                if h in (0, 1) and 0 < g < GROUPS:
+                    group_x(g, h)
+                if valid(i - 1):
+                    quantise_v(i - 1)
+                steps[2]()
+                if h == 2 and 0 < g < GROUPS:
+                    quantise_x(g)
+                if valid(i + 4):
+                    turn_norms(i + 4)
+                if valid(i):
+                    weigh(i)
+                if i in (-2, -1):
+                    for n in (2 * i + 8, 2 * i + 9):
+                        square(n)
+                if i == -1:
+                    for step in split_steps(1, all_heads):
+                        step()
                     wv_grouped = stage.tile([P, TOKENS * PACK], BF16, name="x_grouped", align_bytes=64)
                     x_grouped[0] = stage.tile([P, TOKENS * PACK], BF16, name="x_grouped", align_bytes=64)
                     for rows, grouped, copy in (
                         (wv_raw, wv_grouped, nc.scalar.copy),
                         (x_raw[0], x_grouped[0], nc.vector.tensor_copy),
                     ):
-                        for pair in range(2):
-                            group_rows(turn_rows(rows, pair, psum_qk, "qk"), grouped, pair, copy)
+                        for pair, tag in ((0, "v_acc"), (1, "o_acc")):
+                            group_rows(turn_rows(rows, pair, psum_mx, tag), grouped, pair, copy)
                     quantise(wv_codes[:], wv_scales[:], wv_grouped[:])
                     quantise_x(0)
                     load_x(3)
-                if valid(i + 3):
-                    turn_norms(i + 3)
-                if valid(i + 1):
-                    inverse_root(i + 1)
-                    expand(i + 1)
-                if valid(i + 3):
-                    copy_norms(i + 3)
-                if i == -3:
-                    split_norms(0, slice(HEADS // 2, HEADS), nc.gpsimd)
-                if valid(i + 2):
-                    scores(i + 2, (0,))
-                if valid(i + 2):
-                    project(i + 2)
-                if valid(i - 2):
-                    attend(i - 2)
-                for t, turned_tiles in ((1, (0, 1)), (3, (2,)), (2, (3,))):
-                    if valid(i + 2):
-                        scores(i + 2, (t,))
-                    if valid(i + 4):
-                        turn_qk(i + 4, turned_tiles)
-                if next_x and h in (1, 2):
-                    turn_x(g + 1, h - 1)
-                if valid(i - 1):
-                    quantise_w(i - 1)
-                if valid(i + 1):
-                    expand_last(i + 1)
-                if valid(i):
-                    quantise_v(i)
-                if next_x and h == 3:
-                    quantise_x(g + 1)
-                if valid(i):
-                    weigh(i)
-                if i == -1:
-                    for n in range(HEADS, ON_GPSIMD):
-                        square(n)
-                if ON_GPSIMD <= i + 8 < ALL_HEADS:
-                    sum_folds(i + 8)
                 if ON_GPSIMD <= i + 9 < ALL_HEADS:
-                    square(i + 9)
-                if (i + 5) % HEADS == 0 and HEADS <= i + 5 < ALL_HEADS:
-                    split_norms((i + 5) // HEADS, all_heads, nc.gpsimd)
+                    sum_folds(i + 9)
+                for step in steps[3:]:
+                    step()
+                if ON_GPSIMD <= i + 10 < ALL_HEADS:
+                    square(i + 10)
+                    fold_squares(i + 10)
                 if valid(i + 4) and h == 2 and g + 4 < GROUPS:
                     load_qk(g + 4, 1)
                     load_x(g + 4)

@@ -27,6 +27,7 @@ HEAD_STEP = TILES * P + SLOT
 BY_MATMUL = [0, 1, 3]
 MASKED = -(2.0**95)
 ALL_HEADS = GROUPS * HEADS
+BANK = (0, 1, 2, 1)
 W_BUFS = 3
 VECTOR_COPIES = ALL_HEADS - 13
 ON_GPSIMD = 8
@@ -210,10 +211,8 @@ def tile_networklayer_pb_t_kernel(tc, q_pos, k_pos, x_grp, Wv, bv, out):
             g, h = divmod(n, HEADS)
             folds[n] = [fold.tile([P, GPSIMD_TILES, P >> i], F32, name="fold%d" % i) for i in range(FOLDS + 1)]
             first = h * TILES
-            for source, start, stop in ((q_raw[g], 0, 2), (q_raw[g], 2, 4), (k_raw[g], 4, GPSIMD_TILES)):
-                if stop > start:
-                    rows = source[:, first + start % TILES : first + start % TILES + stop - start, :]
-                    nc.gpsimd.tensor_tensor(out=folds[n][0][:, start:stop, :], in0=rows, in1=rows, op=ALU.mult)
+            rows = q_raw[g][:, first : first + TILES, :]
+            nc.gpsimd.tensor_tensor(out=folds[n][0][:], in0=rows, in1=rows, op=ALU.mult)
             for i in range(FOLDS):
                 half = P >> (i + 1)
                 nc.gpsimd.tensor_tensor(
@@ -254,7 +253,7 @@ def tile_networklayer_pb_t_kernel(tc, q_pos, k_pos, x_grp, Wv, bv, out):
         def turn_norms(n):
             g, h = divmod(n, HEADS)
             norm_psum[n] = psum_tp.tile([P, 2, TILES, P], BF16, name="tp_norms", tag="tp_side")
-            for slot, t in enumerate(BY_MATMUL):
+            for slot, t in enumerate(by_matmul(n)):
                 nc.tensor.transpose(
                     out=norm_psum[n][:, 0, slot, :],
                     in_=split_k[g % 2][:, (h * TILES + t) * P : (h * TILES + t + 1) * P],
@@ -266,9 +265,9 @@ def tile_networklayer_pb_t_kernel(tc, q_pos, k_pos, x_grp, Wv, bv, out):
 
         def copy_norms(n):
             g, h = divmod(n, HEADS)
-            slots = len(BY_MATMUL)
-            k_side[n] = turned.tile([P, slots, P], BF16, name="k_side")
-            nc.scalar.copy(out=k_side[n][:], in_=norm_psum[n][:, 0, 0:slots, :])
+            slots = len(by_matmul(n))
+            k_side[n] = turned.tile([P, TILES, P], BF16, name="k_side")
+            nc.scalar.copy(out=k_side[n][:, 0:slots, :], in_=norm_psum[n][:, 0, 0:slots, :])
             if h == 0 or n in RETURNED:
                 q_side[g] = turned.tile([P, TOKENS], BF16, name="q_side")
                 nc.scalar.copy(
@@ -329,18 +328,21 @@ def tile_networklayer_pb_t_kernel(tc, q_pos, k_pos, x_grp, Wv, bv, out):
                 v_scales[g] = vcode.tile([P, MODEL], U8, name="v_scales", align_bytes=64)
             quantise(v_codes[g][:, cols], v_scales[g][:, cols], v_grouped[n][:].rearrange("p j t -> p (j t)"))
 
+        def by_matmul(n):
+            return BY_MATMUL + [2] * (n % 3 == 0)
+
         def block(n, t):
             width = TOKENS - t * P
             first = 0 if t != 3 else TOKENS - P
-            return scores_psum[n][(0, 1, 2, 1)[t]][:, first : first + width]
+            return scores_psum[n, BANK[t]][:, first : first + width]
 
         def scores(n, tiles):
             g, h = divmod(n, HEADS)
             q_t = qk_turned[n][:, 0, :]
             k_t = qk_turned[n][:, 1, :]
-            if 0 in tiles:
-                scores_psum[n] = [psum_qk.tile([P, TOKENS], F32, name="qk_acc", tag="qk") for bank in range(3)]
             for t in tiles:
+                if BANK[t] == t:
+                    scores_psum[n, t] = psum_qk.tile([P, TOKENS], F32, name="qk_acc", tag="qk")
                 acc = block(n, t)
                 nc.tensor.matmul(
                     out=acc, lhsT=k_t[:, t * P : (t + 1) * P], rhs=q_t[:, t * P : TOKENS], start=True, stop=False
@@ -349,9 +351,9 @@ def tile_networklayer_pb_t_kernel(tc, q_pos, k_pos, x_grp, Wv, bv, out):
                     nc.tensor.matmul(
                         out=acc[:, 0:P], lhsT=mask[:], rhs=ident_f[:], is_transpose=True, start=False, stop=False
                     )
-                if t in BY_MATMUL:
+                if t in by_matmul(n):
                     nc.tensor.matmul(
-                        out=acc, lhsT=k_side[n][:, BY_MATMUL.index(t), :], rhs=q_side[g][:, t * P : TOKENS], start=False, stop=True
+                        out=acc, lhsT=k_side[n][:, by_matmul(n).index(t), :], rhs=q_side[g][:, t * P : TOKENS], start=False, stop=True
                     )
                 else:
                     for u in range(t, TILES):
@@ -373,7 +375,7 @@ def tile_networklayer_pb_t_kernel(tc, q_pos, k_pos, x_grp, Wv, bv, out):
                     in_=block(n, t),
                     func=ACT.Abs_reciprocal_sqrt,
                     scale=-2.0,
-                    bias=EPS if t in BY_MATMUL else norm_sums[g][:, h, 1, t : t + 1],
+                    bias=EPS if t in by_matmul(n) else norm_sums[g][:, h, 1, t : t + 1],
                 )
 
         def expand(n):
@@ -382,12 +384,20 @@ def tile_networklayer_pb_t_kernel(tc, q_pos, k_pos, x_grp, Wv, bv, out):
                 nc.vector.scalar_tensor_tensor(
                     out=row, in0=row, scalar=0.5, in1=block(n, t), op0=ALU.add, op1=ALU.mult
                 )
-            row = work[n][:, 2, 2 * P : TOKENS]
-            nc.vector.tensor_scalar(out=row, in0=row, scalar1=INV_EPS, scalar2=0.5, op0=ALU.min, op1=ALU.add)
+
+        def lift(n):
+            if 2 not in by_matmul(n):
+                row = work[n][:, 2, 2 * P : TOKENS]
+                nc.vector.tensor_scalar(out=row, in0=row, scalar1=INV_EPS, scalar2=0.5, op0=ALU.min, op1=ALU.add)
 
         def expand_last(n):
             g, h = divmod(n, HEADS)
             row = work[n][:, 2, 2 * P : TOKENS]
+            if 2 in by_matmul(n):
+                nc.vector.scalar_tensor_tensor(
+                    out=row, in0=row, scalar=0.5, in1=block(n, 2), op0=ALU.add, op1=ALU.mult
+                )
+                return
             nc.vector.scalar_tensor_tensor(
                 out=row,
                 in0=block(n, 2),
@@ -455,8 +465,8 @@ def tile_networklayer_pb_t_kernel(tc, q_pos, k_pos, x_grp, Wv, bv, out):
         load_qk(1, 1)
         nc.sync.dma_start(out=wv_raw[:], in_=Wv.rearrange("(t p) k -> p t k", p=P))
         load_x(0)
-        nc.sync.dma_start(out=bias[:], in_=bv.partition_broadcast(P))
         load_qk(2, 1)
+        nc.sync.dma_start(out=bias[:], in_=bv.partition_broadcast(P))
         load_x(1)
         load_qk(3, 1)
         load_x(2)
@@ -490,18 +500,23 @@ def tile_networklayer_pb_t_kernel(tc, q_pos, k_pos, x_grp, Wv, bv, out):
                         nc.vector.memset(w_tile[:].rearrange("p b t -> p (b t)").bitcast(U32), 0)
                 if valid(i + 1):
                     inverse_root(i + 1)
-                if valid(i + 1):
-                    expand(i + 1)
                 if valid(i + 3):
                     copy_norms(i + 3)
                 if valid(i + 2):
                     scores(i + 2, (0,))
-                if h in (0, 1) and 0 < g < GROUPS:
-                    turn_x(g, h)
                 if valid(i):
                     project(i)
                 if valid(i - 2):
                     attend(i - 2)
+                if h in (0, 1) and 0 < g < GROUPS:
+                    turn_x(g, h)
+                if valid(i + 1):
+                    expand(i + 1)
+                if h in (0, 1) and 0 < g < GROUPS:
+                    group_x(g, h)
+                if valid(i + 1):
+                    lift(i + 1)
+                steps[0]()
                 if valid(i + 2):
                     scores(i + 2, (1,))
                 if valid(i + 2):
@@ -512,17 +527,18 @@ def tile_networklayer_pb_t_kernel(tc, q_pos, k_pos, x_grp, Wv, bv, out):
                     turn_qk(i + 4, range(TILES))
                 if valid(i - 1):
                     quantise_w(i - 1)
-                steps[0]()
+                steps[1]()
                 if valid(i + 1):
                     expand_last(i + 1)
-                steps[1]()
-                if h in (0, 1) and 0 < g < GROUPS:
-                    group_x(g, h)
+                steps[2]()
                 if valid(i - 1):
                     quantise_v(i - 1)
-                steps[2]()
+                steps[3]()
                 if h == 2 and 0 < g < GROUPS:
                     quantise_x(g)
+                steps[4]()
+                steps[5]()
+                steps[6]()
                 if valid(i + 4):
                     turn_norms(i + 4)
                 if valid(i):
@@ -546,8 +562,6 @@ def tile_networklayer_pb_t_kernel(tc, q_pos, k_pos, x_grp, Wv, bv, out):
                     load_x(3)
                 if ON_GPSIMD <= i + 9 < ALL_HEADS:
                     sum_folds(i + 9)
-                for step in steps[3:]:
-                    step()
                 if ON_GPSIMD <= i + 10 < ALL_HEADS:
                     square(i + 10)
                     fold_squares(i + 10)

from contextlib import ExitStack

import concourse.mybir as mybir
from concourse.masks import make_identity

F32 = mybir.dt.float32
BF16 = mybir.dt.bfloat16
U32 = mybir.dt.uint32
U8 = mybir.dt.uint8
FP8X4 = mybir.dt.float8_e4m3fn_x4
ACT = mybir.ActivationFunctionType
ALU = mybir.AluOpType

P = 128
GROUPS = 8
HEADS = 4
TOKENS = 512
TILES = TOKENS // P
MODEL = 512
PACK = 4
EPS = 1.0e-12
INV_EPS = 1.0e6
SPLIT = 3
SLOT = 32
KEY_ROW = 16
HEAD_STEP = TILES * P + SLOT
BY_MATMUL = [0, 1, 3]
MASKED = -(2.0**95)
ALL_HEADS = GROUPS * HEADS
BANK = (0, 1, 2, 1)
W_BUFS = 3
VECTOR_COPIES = ALL_HEADS - 13
ON_GPSIMD = 8
RETURNED = (2,)
FOLDS = 1
GPSIMD_TILES = 4
RUN = 4

FLOPS = 3 * 2 * GROUPS * TOKENS * MODEL * MODEL


def tile_networklayer_pb_t_kernel(tc, q_pos, k_pos, x_grp, Wv, bv, out):
    nc = tc.nc
    with ExitStack() as ctx:
        const = ctx.enter_context(tc.tile_pool(name="const", bufs=1))
        raw = ctx.enter_context(tc.tile_pool(name="raw", bufs=4))
        stage = ctx.enter_context(tc.tile_pool(name="stage", bufs=2))
        norms = ctx.enter_context(tc.tile_pool(name="norms", bufs=4))
        fold = ctx.enter_context(tc.tile_pool(name="fold", bufs=1))
        turned = ctx.enter_context(tc.tile_pool(name="turned", bufs=4))
        dist = ctx.enter_context(tc.tile_pool(name="dist", bufs=3))
        wfirst = ctx.enter_context(tc.tile_pool(name="wfirst", bufs=3))
        wcode = ctx.enter_context(tc.tile_pool(name="wcode", bufs=3))
        vcode = ctx.enter_context(tc.tile_pool(name="vcode", bufs=3))
        result = ctx.enter_context(tc.tile_pool(name="result", bufs=2))
        psum_qk = ctx.enter_context(tc.psum_pool(name="psum_qk", bufs=4))
        psum_tp = ctx.enter_context(tc.psum_pool(name="psum_tp", bufs=1))
        psum_mx = ctx.enter_context(tc.psum_pool(name="psum_mx", bufs=1))

        ident_b = const.tile([P, P], BF16, name="ident_b")
        make_identity(nc, ident_b[:])
        ident_f = const.tile([P, P], F32, name="ident_f")
        make_identity(nc, ident_f[:])
        mask = const.tile([P, P], F32, name="mask")
        nc.gpsimd.memset(mask[:], 0.0)
        nc.gpsimd.affine_select(
            out=mask[:],
            in_=mask[:],
            pattern=[[-1, P]],
            compare_op=ALU.is_ge,
            fill=MASKED,
            base=0,
            channel_multiplier=1,
        )
        allowed = const.tile([P, P], BF16, name="allowed")
        nc.gpsimd.memset(allowed[:], 1.0)
        nc.gpsimd.affine_select(
            out=allowed[:],
            in_=allowed[:],
            pattern=[[1, P]],
            compare_op=ALU.is_ge,
            fill=0.0,
            base=0,
            channel_multiplier=-1,
        )
        one = const.tile([P, 1], F32, name="one")
        nc.vector.memset(one[:], 1.0)
        nc.scalar.activation(out=one[:], in_=one[:], func=ACT.Abs_reciprocal_sqrt)
        bias = const.tile([P, MODEL], BF16, name="bias")
        squares = const.tile([P, HEADS, 2 * TILES, P], F32, name="squares")
        weights = [
            const.tile([P, TOKENS, PACK], BF16, name="weights%d" % i, align_bytes=64)
            for i in range(W_BUFS)
        ]
        split_q = [const.tile([P, TILES, P], BF16, name="split_q%d" % i) for i in range(2)]
        split_k = [const.tile([P, HEADS * HEAD_STEP], BF16, name="split_k%d" % i) for i in range(2)]

        def query_rows(i, first, heads):
            rows = split_q[i][:].rearrange("p u (h s) -> p h u s", s=SLOT)
            return rows[:, heads, :, first : first + SPLIT]

        def key_rows(i, first, heads):
            rows = split_k[i][:].rearrange("p (h x) -> p h x", x=HEAD_STEP)[:, :, 0 : TILES * P]
            return rows.rearrange("p h (t c) -> p h t c", c=P)[:, heads, :, first : first + SPLIT]

        all_heads = slice(0, HEADS)
        for i in range(2):
            nc.vector.memset(split_q[i][:].rearrange("p u c -> p (u c)").bitcast(U32), 0)
            nc.vector.memset(split_k[i][:].bitcast(U32), 0)
            nc.vector.memset(query_rows(i, KEY_ROW, all_heads), -0.5)
            nc.vector.memset(key_rows(i, 0, all_heads), -0.5)
        wv_codes = const.tile([P, MODEL], U32, name="wv_codes", align_bytes=64)
        wv_scales = const.tile([P, MODEL], U8, name="wv_scales", align_bytes=64)

        q_raw = {}
        k_raw = {}
        x_raw = {}
        q_side = {}
        k_side = {}
        norm_psum = {}
        x_psum = {}
        x_grouped = {}
        x_codes = {}
        x_scales = {}
        v_grouped = {}
        v_codes = {}
        v_scales = {}
        norm_sums = {}
        half_norms = {}
        folds = {}
        qk_psum = {}
        qk_turned = {}
        scores_psum = {}
        work = {}
        w_codes = {}
        w_scales = {}
        v_psum = {}
        o_psum = {}
        o_rows = {}

        def load_x(g):
            x_raw[g] = raw.tile([P, TILES, MODEL], BF16, name="x_raw")
            nc.sync.dma_start(out=x_raw[g][:], in_=x_grp[g].rearrange("(t p) k -> p t k", p=P))

        def load_qk(g, pieces):
            k_raw[g] = raw.tile([P, HEADS * TILES, P], BF16, name="k_raw")
            q_raw[g] = raw.tile([P, HEADS * TILES, P], BF16, name="q_raw")
            heads = HEADS // pieces
            for first in range(0, HEADS, heads):
                rows = slice(first * TILES, (first + heads) * TILES)
                for target, source in ((k_raw[g], k_pos[g]), (q_raw[g], q_pos[g])):
                    nc.sync.dma_start(
                        out=target[:, rows, :],
                        in_=source[first : first + heads].rearrange("h (u p) d -> p (h u) d", p=P),
                    )

        def turn_rows(rows, pair, pool, tag):
            words = rows[:].bitcast(F32)
            tp = pool.tile([P, 2, 2 * P], F32, name="tp_words", tag=tag)
            for i in range(2):
                for u in range(2):
                    nc.tensor.transpose(
                        out=tp[:, u, i * P : (i + 1) * P],
                        in_=words[:, 2 * pair + i, u * P : (u + 1) * P],
                        identity=ident_f[:],
                    )
            return tp

        def group_rows(tp, grouped, pair, copy):
            grouped_words = grouped[:].bitcast(F32).rearrange("p (r u) -> p r u", u=2)
            copy(
                out=grouped_words[:, 2 * pair * P : 2 * (pair + 1) * P, :],
                in_=tp[:].rearrange("p u r -> p r u"),
            )

        def quantise(codes, scales, grouped):
            nc.vector.quantize_mx(out=codes.bitcast(FP8X4), scales=scales, in_=grouped)

        def turn_x(g, pair):
            x_psum[g] = turn_rows(x_raw[g], pair, psum_tp, "tp_side")

        def group_x(g, pair):
            if pair == 0:
                x_grouped[g] = stage.tile([P, TOKENS * PACK], BF16, name="x_grouped", align_bytes=64)
            group_rows(x_psum[g], x_grouped[g], pair, nc.vector.tensor_copy)

        def quantise_x(g):
            x_codes[g] = stage.tile([P, TOKENS], U32, name="x_codes", align_bytes=64)
            x_scales[g] = stage.tile([P, TOKENS], U8, name="x_scales", align_bytes=64)
            quantise(x_codes[g][:], x_scales[g][:], x_grouped[g][:])

        def square(n):
            g, h = divmod(n, HEADS)
            if h == 0:
                norm_sums[g] = norms.tile([P, HEADS, 2, TILES], F32, name="norm_sums")
            for side, source in ((1, k_raw[g]), (0, q_raw[g])):
                for u in range(TILES):
                    rows = source[:, h * TILES + u, :]
                    unused = squares[:, h, side * TILES + u, :]
                    total = norm_sums[g][:, h, side, u : u + 1]
                    if n >= ON_GPSIMD and side * TILES + u < GPSIMD_TILES:
                        continue
                    if side == 0 and h < 2:
                        nc.vector.scalar_tensor_tensor(
                            out=unused, in0=rows, scalar=1.0, in1=rows, op0=ALU.mult, op1=ALU.mult, accum_out=total
                        )
                    else:
                        nc.scalar.activation(out=unused, in_=rows, func=ACT.Square, accum_out=total)

        def fold_squares(n):
            g, h = divmod(n, HEADS)
            folds[n] = [fold.tile([P, GPSIMD_TILES, P >> i], F32, name="fold%d" % i) for i in range(FOLDS + 1)]
            first = h * TILES
            rows = q_raw[g][:, first : first + TILES, :]
            nc.gpsimd.tensor_tensor(out=folds[n][0][:], in0=rows, in1=rows, op=ALU.mult)
            for i in range(FOLDS):
                half = P >> (i + 1)
                nc.gpsimd.tensor_tensor(
                    out=folds[n][i + 1][:],
                    in0=folds[n][i][:, :, 0:half],
                    in1=folds[n][i][:, :, half : 2 * half],
                    op=ALU.add,
                )

        def sum_folds(n):
            g, h = divmod(n, HEADS)
            sums = norm_sums[g][:, h].rearrange("p i u -> p (i u)")
            nc.vector.tensor_reduce(
                out=sums[:, 0:GPSIMD_TILES], in_=folds[n][FOLDS][:], axis=mybir.AxisListType.X, op=ALU.add
            )

        def split_steps(g, heads):
            if heads.start == 0:
                half_norms[g] = norms.tile([P, HEADS, 2, TILES], F32, name="half_norms")
            sums = norm_sums[g][:, heads]
            all_terms = norms.tile([P, SPLIT, HEADS, 2, TILES], BF16, name="terms")
            terms = [all_terms[:, i, heads] for i in range(SPLIT)]
            rest = norms.tile([P, HEADS, 2, TILES], F32, name="rest")[:, heads]

            def place(side, rows):
                nc.vector.tensor_copy(out=rows, in_=all_terms[:, :, heads, side, :].rearrange("p i h u -> p h u i"))

            return [
                lambda: nc.vector.tensor_copy(out=terms[0], in_=sums),
                lambda: nc.vector.tensor_tensor(out=rest, in0=sums, in1=terms[0], op=ALU.subtract),
                lambda: nc.vector.tensor_copy(out=terms[1], in_=rest),
                lambda: nc.vector.tensor_tensor(out=terms[2], in0=rest, in1=terms[1], op=ALU.subtract),
                lambda: place(0, query_rows(g % 2, 0, heads)),
                lambda: place(1, key_rows(g % 2, KEY_ROW, heads)),
                lambda: nc.vector.tensor_scalar_mul(out=half_norms[g][:, heads], in0=sums, scalar1=-0.5),
            ]

        def turn_norms(n):
            g, h = divmod(n, HEADS)
            norm_psum[n] = psum_tp.tile([P, 2, TILES, P], BF16, name="tp_norms", tag="tp_side")
            for slot, t in enumerate(by_matmul(n)):
                nc.tensor.transpose(
                    out=norm_psum[n][:, 0, slot, :],
                    in_=split_k[g % 2][:, (h * TILES + t) * P : (h * TILES + t + 1) * P],
                    identity=ident_b[:],
                )
            if h == 0 or n in RETURNED:
                for u in range(TILES):
                    nc.tensor.transpose(out=norm_psum[n][:, 1, u, :], in_=split_q[g % 2][:, u, :], identity=ident_b[:])

        def copy_norms(n):
            g, h = divmod(n, HEADS)
            slots = len(by_matmul(n))
            k_side[n] = turned.tile([P, TILES, P], BF16, name="k_side")
            nc.scalar.copy(out=k_side[n][:, 0:slots, :], in_=norm_psum[n][:, 0, 0:slots, :])
            if h == 0 or n in RETURNED:
                q_side[g] = turned.tile([P, TOKENS], BF16, name="q_side")
                nc.scalar.copy(
                    out=q_side[g][:], in_=norm_psum[n][:, 1].rearrange("p u b -> p (u b)")
                )

        def turn_qk(n, tiles):
            g, h = divmod(n, HEADS)
            if 0 in tiles:
                qk_psum[n] = psum_tp.tile([P, 2 * TILES, P], BF16, name="tp_qk", tag="tp_qk")
            for i, source in enumerate((q_raw[g], k_raw[g])):
                for u in tiles:
                    nc.tensor.transpose(
                        out=qk_psum[n][:, i * TILES + u, :],
                        in_=source[:, h * TILES + u, :],
                        identity=ident_b[:],
                    )

        def copy_qk(n):
            qk_turned[n] = turned.tile([P, 2, TOKENS], BF16, name="qk_turned")
            nc.vector.tensor_copy(
                out=qk_turned[n][:].rearrange("p a b -> p (a b)"),
                in_=qk_psum[n][:].rearrange("p i b -> p (i b)"),
            )

        def project(n):
            g, h = divmod(n, HEADS)
            cols = slice(h * P, (h + 1) * P)
            v_psum[n] = psum_mx.tile([P, TILES, P], F32, name="v_acc")
            for t in range(TILES):
                rows = slice(t * P, (t + 1) * P)
                nc.tensor.matmul_mx(
                    out=v_psum[n][:, t, :],
                    lhsT=x_codes[g][:, rows].bitcast(FP8X4),
                    lhsT_scale=x_scales[g][:, rows],
                    rhs=wv_codes[:, cols].bitcast(FP8X4),
                    rhs_scale=wv_scales[:, cols],
                    start=True,
                    stop=True,
                )

        def add_bias(n):
            g, h = divmod(n, HEADS)
            cols = slice(h * P, (h + 1) * P)
            v_grouped[n] = stage.tile([P, P, PACK], BF16, name="v_grouped", align_bytes=64)
            nc.vector.tensor_tensor(
                out=v_grouped[n][:],
                in0=v_psum[n][:].rearrange("p t j -> p j t"),
                in1=bias[:, cols].unsqueeze(2).to_broadcast([P, P, PACK]),
                op=ALU.add,
            )

        def quantise_v(n):
            g, h = divmod(n, HEADS)
            cols = slice(h * P, (h + 1) * P)
            if h == 0:
                v_codes[g] = vcode.tile([P, MODEL], U32, name="v_codes", align_bytes=64)
                v_scales[g] = vcode.tile([P, MODEL], U8, name="v_scales", align_bytes=64)
            quantise(v_codes[g][:, cols], v_scales[g][:, cols], v_grouped[n][:].rearrange("p j t -> p (j t)"))

        def by_matmul(n):
            return BY_MATMUL + [2] * (n % 3 == 0)

        def block(n, t):
            width = TOKENS - t * P
            first = 0 if t != 3 else TOKENS - P
            return scores_psum[n, BANK[t]][:, first : first + width]

        def scores(n, tiles):
            g, h = divmod(n, HEADS)
            q_t = qk_turned[n][:, 0, :]
            k_t = qk_turned[n][:, 1, :]
            for t in tiles:
                if BANK[t] == t:
                    scores_psum[n, t] = psum_qk.tile([P, TOKENS], F32, name="qk_acc", tag="qk")
                acc = block(n, t)
                nc.tensor.matmul(
                    out=acc, lhsT=k_t[:, t * P : (t + 1) * P], rhs=q_t[:, t * P : TOKENS], start=True, stop=False
                )
                if t > 0:
                    nc.tensor.matmul(
                        out=acc[:, 0:P], lhsT=mask[:], rhs=ident_f[:], is_transpose=True, start=False, stop=False
                    )
                if t in by_matmul(n):
                    nc.tensor.matmul(
                        out=acc, lhsT=k_side[n][:, by_matmul(n).index(t), :], rhs=q_side[g][:, t * P : TOKENS], start=False, stop=True
                    )
                else:
                    for u in range(t, TILES):
                        nc.tensor.matmul(
                            out=acc[:, (u - t) * P : (u - t + 1) * P],
                            lhsT=half_norms[g][:, h, 0, u : u + 1].to_broadcast([P, P]),
                            rhs=ident_f[:],
                            is_transpose=True,
                            start=False,
                            stop=(u == TILES - 1),
                        )

        def inverse_root(n):
            g, h = divmod(n, HEADS)
            work[n] = dist.tile([P, TILES, TOKENS], F32, name="work")
            for t in (0, 1, 3, 2):
                nc.scalar.activation(
                    out=work[n][:, t, t * P : TOKENS],
                    in_=block(n, t),
                    func=ACT.Abs_reciprocal_sqrt,
                    scale=-2.0,
                    bias=EPS if t in by_matmul(n) else norm_sums[g][:, h, 1, t : t + 1],
                )

        def expand(n):
            for t in BY_MATMUL:
                row = work[n][:, t, t * P : TOKENS]
                nc.vector.scalar_tensor_tensor(
                    out=row, in0=row, scalar=0.5, in1=block(n, t), op0=ALU.add, op1=ALU.mult
                )

        def lift(n):
            if 2 not in by_matmul(n):
                row = work[n][:, 2, 2 * P : TOKENS]
                nc.vector.tensor_scalar(out=row, in0=row, scalar1=INV_EPS, scalar2=0.5, op0=ALU.min, op1=ALU.add)

        def expand_last(n):
            g, h = divmod(n, HEADS)
            row = work[n][:, 2, 2 * P : TOKENS]
            if 2 in by_matmul(n):
                nc.vector.scalar_tensor_tensor(
                    out=row, in0=row, scalar=0.5, in1=block(n, 2), op0=ALU.add, op1=ALU.mult
                )
                return
            nc.vector.scalar_tensor_tensor(
                out=row,
                in0=block(n, 2),
                scalar=half_norms[g][:, h, 1, 2:3],
                in1=row,
                op0=ALU.add,
                op1=ALU.mult,
            )

        def weigh(n):
            w_tile = weights[n % W_BUFS]
            first = wfirst.tile([P, P], BF16, name="first")
            nc.scalar.activation(
                out=first[:], in_=work[n][:, 0, 0:P], func=ACT.Abs_reciprocal_sqrt, scale=-4.0, bias=1.0
            )
            for u in range(1, TILES):
                cols = slice(u * P, (u + 1) * P)
                nc.scalar.activation(
                    out=w_tile[:, cols, 0 : u + 1].rearrange("p (c i) t -> p c t i", i=RUN),
                    in_=work[n][:, 0 : u + 1, cols].rearrange("p t (c i) -> p c t i", i=RUN),
                    func=ACT.Abs_reciprocal_sqrt,
                    scale=-4.0,
                    bias=1.0,
                )
            nc.gpsimd.tensor_tensor(out=w_tile[:, 0:P, 0], in0=first[:], in1=allowed[:], op=ALU.mult)

        def quantise_w(n):
            w_codes[n] = wcode.tile([P, TOKENS], U32, name="w_codes", align_bytes=64)
            w_scales[n] = wcode.tile([P, TOKENS], U8, name="w_scales", align_bytes=64)
            quantise(w_codes[n][:], w_scales[n][:], weights[n % W_BUFS][:].rearrange("p b t -> p (b t)"))

        def attend(n):
            g, h = divmod(n, HEADS)
            cols = slice(h * P, (h + 1) * P)
            o_psum[n] = psum_mx.tile([P, TILES, P], F32, name="o_acc")
            for u in range(TILES):
                rows = slice(u * P, (u + 1) * P)
                nc.tensor.matmul_mx(
                    out=o_psum[n][:, u, :],
                    lhsT=w_codes[n][:, rows].bitcast(FP8X4),
                    lhsT_scale=w_scales[n][:, rows],
                    rhs=v_codes[g][:, cols].bitcast(FP8X4),
                    rhs_scale=v_scales[g][:, cols],
                    start=True,
                    stop=True,
                )

        def copy_out(n):
            g, h = divmod(n, HEADS)
            cols = slice(h * P, (h + 1) * P)
            if h == 0:
                o_rows[g] = result.tile([P, TILES, MODEL], F32, name="o_rows")
            if n < VECTOR_COPIES and h == 0:
                nc.vector.tensor_copy(out=o_rows[g][:, :, cols], in_=o_psum[n][:])
            else:
                nc.scalar.copy(out=o_rows[g][:, :, cols], in_=o_psum[n][:])
            target = out[g].rearrange("(u p) j -> p u j", p=P)
            if g == GROUPS - 1:
                nc.sync.dma_start(out=target[:, :, cols], in_=o_rows[g][:, :, cols])
            elif h == HEADS - 1:
                nc.sync.dma_start(out=target, in_=o_rows[g][:])

        wv_raw = raw.tile([P, TILES, MODEL], BF16, name="x_raw")
        load_qk(0, 2)
        load_qk(1, 1)
        nc.sync.dma_start(out=wv_raw[:], in_=Wv.rearrange("(t p) k -> p t k", p=P))
        load_x(0)
        load_qk(2, 1)
        nc.sync.dma_start(out=bias[:], in_=bv.partition_broadcast(P))
        load_x(1)
        load_qk(3, 1)
        load_x(2)

        def valid(n):
            return 0 <= n < ALL_HEADS

        with tc.manual_schedule():
            for n in range(HEADS // 2):
                square(n)
            for step in split_steps(0, slice(0, HEADS // 2)):
                step()
            for i in range(-4, ALL_HEADS + 4):
                g, h = divmod(i + 3, HEADS)
                steps = []
                if (i + 5) % HEADS == 0 and 2 * HEADS <= i + 5 < ALL_HEADS:
                    steps = split_steps((i + 5) // HEADS, all_heads)
                steps = steps + [lambda: None] * (7 - len(steps))
                if valid(i - 3):
                    copy_out(i - 3)
                if valid(i - 1):
                    add_bias(i - 1)
                if valid(i + 3):
                    copy_qk(i + 3)
                if i == -3:
                    for n in range(HEADS // 2, HEADS):
                        square(n)
                    for step in split_steps(0, slice(HEADS // 2, HEADS)):
                        step()
                    for w_tile in weights:
                        nc.vector.memset(w_tile[:].rearrange("p b t -> p (b t)").bitcast(U32), 0)
                if valid(i + 1):
                    inverse_root(i + 1)
                if valid(i + 3):
                    copy_norms(i + 3)
                if valid(i + 2):
                    scores(i + 2, (0,))
                if valid(i):
                    project(i)
                if valid(i - 2):
                    attend(i - 2)
                if h in (0, 1) and 0 < g < GROUPS:
                    turn_x(g, h)
                if valid(i + 1):
                    expand(i + 1)
                if h in (0, 1) and 0 < g < GROUPS:
                    group_x(g, h)
                if valid(i + 1):
                    lift(i + 1)
                steps[0]()
                if valid(i + 2):
                    scores(i + 2, (1,))
                if valid(i + 2):
                    scores(i + 2, (3,))
                if valid(i + 2):
                    scores(i + 2, (2,))
                if valid(i + 4):
                    turn_qk(i + 4, range(TILES))
                if valid(i - 1):
                    quantise_w(i - 1)
                steps[1]()
                if valid(i + 1):
                    expand_last(i + 1)
                steps[2]()
                if valid(i - 1):
                    quantise_v(i - 1)
                steps[3]()
                if h == 2 and 0 < g < GROUPS:
                    quantise_x(g)
                steps[4]()
                steps[5]()
                steps[6]()
                if valid(i + 4):
                    turn_norms(i + 4)
                if valid(i):
                    weigh(i)
                if i in (-2, -1):
                    for n in (2 * i + 8, 2 * i + 9):
                        square(n)
                if i == -1:
                    for step in split_steps(1, all_heads):
                        step()
                    wv_grouped = stage.tile([P, TOKENS * PACK], BF16, name="x_grouped", align_bytes=64)
                    x_grouped[0] = stage.tile([P, TOKENS * PACK], BF16, name="x_grouped", align_bytes=64)
                    for rows, grouped, copy in (
                        (wv_raw, wv_grouped, nc.scalar.copy),
                        (x_raw[0], x_grouped[0], nc.vector.tensor_copy),
                    ):
                        for pair, tag in ((0, "v_acc"), (1, "o_acc")):
                            group_rows(turn_rows(rows, pair, psum_mx, tag), grouped, pair, copy)
                    quantise(wv_codes[:], wv_scales[:], wv_grouped[:])
                    quantise_x(0)
                    load_x(3)
                if ON_GPSIMD <= i + 9 < ALL_HEADS:
                    sum_folds(i + 9)
                if ON_GPSIMD <= i + 10 < ALL_HEADS:
                    square(i + 10)
                    fold_squares(i + 10)
                if valid(i + 4) and h == 2 and g + 4 < GROUPS:
                    load_qk(g + 4, 1)
                    load_x(g + 4)
